import numpy as np
import ml_dtypes


def mxq(x, axis, fmt="e4m3"):
    dtype, down = {"e4m3": (ml_dtypes.float8_e4m3fn, 7), "e5m2": (ml_dtypes.float8_e5m2, 14)}[fmt]
    v = np.moveaxis(np.asarray(x, np.float32).astype(ml_dtypes.bfloat16).astype(np.float64), axis, -1)
    blocks = v.reshape(v.shape[:-1] + (-1, 32))
    amax = np.abs(blocks).max(-1, keepdims=True)
    byte = np.maximum(np.where(amax > 0, np.frexp(amax)[1] - 1 + 127, 0) - down, 1)
    scale = np.exp2(byte - 127.0)
    codes = (blocks / scale).astype(np.float32).astype(dtype).astype(np.float64)
    return np.moveaxis((codes * scale).reshape(v.shape), -1, axis)


WIDE = False


def mx_kscale(k):
    if not WIDE:
        return np.ones(k)
    levels = np.array([10, -10, 5, -5, 0])
    if k % 512:
        return np.exp2(np.random.permutation(np.resize(levels, k // 32))).repeat(32)
    a = np.empty((k // 512, 16))
    for p in range(k // 512):
        a[p, :8] = np.random.permutation(np.resize(levels, 8))
        for g in range(8):
            far = levels[np.abs(levels - a[p, g]) >= 10]
            a[p, g + 8] = far[np.random.randint(len(far))]
    return np.exp2(a.ravel()).repeat(32)


BF16 = ml_dtypes.bfloat16


def bf(x):
    return np.asarray(x, np.float32).astype(BF16)


def f64(x):
    return np.asarray(x).astype(np.float64)


B, T, C, NH, H = 2, 256, 2048, 16, 128
HH = H // 2
EPS = 2.0 ** -23


def heads(y):
    return y.reshape(B, T, NH, H).transpose(0, 2, 1, 3)


def rope(y, sin, cos):
    y1, y2 = y[..., :HH], y[..., HH:]
    s = sin[None, None, :, :]
    c = cos[None, None, :, :]
    return np.concatenate([y1 * c - y2 * s, y1 * s + y2 * c], axis=-1)


def rmsnorm(y, w):
    ms = np.mean(np.square(y), axis=-1, keepdims=True)
    return y * (1.0 / np.sqrt(ms + EPS)) * w


def draw0():
    s = mx_kscale(C)
    ang = np.arange(T)[:, None] * (1.0 / 10000.0 ** (np.arange(0, H, 2) / H))[None, :]
    return {"x": bf(np.random.standard_normal((B, T, C)) * s),
            "sin": bf(np.sin(ang)),
            "cos": bf(np.cos(ang)),
            "Wq": bf(np.random.standard_normal((NH * H, C)) / np.sqrt(C) / s[None, :]),
            "Wk": bf(np.random.standard_normal((NH * H, C)) / np.sqrt(C) / s[None, :]),
            "q_norm_w": bf(1.0 + 0.1 * np.random.standard_normal(H)),
            "k_norm_w": bf(1.0 + 0.1 * np.random.standard_normal(H))}


def core(x, sin, cos, Wq, Wk, q_norm_w, k_norm_w):
    xq = mxq(f64(x), 2, "e4m3")
    q = heads(xq @ mxq(f64(Wq), 1, "e4m3").T)
    k = heads(xq @ mxq(f64(Wk), 1, "e4m3").T)
    q = rmsnorm(rope(q, f64(sin), f64(cos)), f64(q_norm_w))
    k = rmsnorm(rope(k, f64(sin), f64(cos)), f64(k_norm_w))
    return q, k


def e4m3fn_bytes(y):
    return np.clip(np.asarray(y, np.float64), -448.0, 448.0).astype(np.float32).astype(ml_dtypes.float8_e4m3fn).view(np.uint8)


def e4m3fn_values(b):
    return np.asarray(b, np.uint8).view(ml_dtypes.float8_e4m3fn).astype(np.float64)


def setup_inputs():
    d = draw0()
    x0 = np.asarray(d['Wq']).astype(np.float64)
    s = (np.max(np.abs(x0), axis=(0,), keepdims=True) / 448.0).astype(np.float32)
    out = {}
    for k, v in d.items():
        if k == 'Wq':
            out['Wq_bytes'] = e4m3fn_bytes(x0 / s.astype(np.float64))
            out['Wq_scale'] = s
        else:
            out[k] = v
    return out


def reference(x, sin, cos, Wq_bytes, Wq_scale, Wk, q_norm_w, k_norm_w):
    return core(x, sin, cos, e4m3fn_values(Wq_bytes) * Wq_scale.astype(np.float64), Wk, q_norm_w, k_norm_w)

@@ -1,0 +1,432 @@
+from contextlib import ExitStack
+
+import concourse.mybir as mybir
+from concourse.masks import make_identity
+
+FLOPS = 2 * 512 * 4096 * 2048
+
+F32 = mybir.dt.float32
+BF16 = mybir.dt.bfloat16
+U32 = mybir.dt.uint32
+U8 = mybir.dt.uint8
+FP8 = mybir.dt.float8_e4m3fn
+FP8X4 = mybir.dt.float8_e4m3fn_x4
+ALU = mybir.AluOpType
+ACT = mybir.ActivationFunctionType
+
+P = 128
+K = 2048
+K_PASS = 512
+PASSES = K // K_PASS
+TOKEN_TILES = 4
+HEAD = 128
+HALF = HEAD // 2
+GROUP_HEADS = 4
+GROUP = GROUP_HEADS * HEAD
+EPS = 2.0 ** -23
+FILL = [6, 7, 8, 9, 10, 12, 12, 12, 12]
+WARM_START = 4
+WARM = 2
+
+GROUPS = [("q", 0), ("k", 0), ("k", 1), ("q", 1), ("k", 2), ("q", 2), ("k", 3), ("q", 3)]
+LOAD_ORDER = [("q", 1), ("k", 0), ("k", 1), ("q", 2), ("k", 2), ("q", 3), ("k", 3)]
+
+
+def tile_attention_pa_kernel(
+    tc, x, sin, cos, Wq_bytes, Wq_scale, Wk, q_norm_w, k_norm_w, out_0, out_1
+):
+    nc = tc.nc
+    n_groups = len(GROUPS)
+
+    with ExitStack() as ctx:
+        const = ctx.enter_context(tc.tile_pool(name="const", bufs=1))
+        raw = ctx.enter_context(tc.tile_pool(name="raw", bufs=1))
+        work = ctx.enter_context(tc.tile_pool(name="work", bufs=2))
+        psum = ctx.enter_context(tc.psum_pool(name="psum", bufs=1))
+        ctx.enter_context(tc.manual_schedule())
+
+        scale_rows = const.tile([P, P], F32, name="scale_rows")
+        nc.vector.memset(scale_rows[:], 0.0)
+        nc.scalar.dma_start(
+            out=scale_rows[0 : K // P, :], in_=Wq_scale.rearrange("o (m p) -> (o m) p", p=P)
+        )
+
+        first_bytes = []
+        for g in range(PASSES):
+            t = raw.tile([P, GROUP_HEADS, K_PASS], U8, name="first_bytes%d" % g)
+            nc.sync.dma_start(
+                out=t[:],
+                in_=Wq_bytes[0:GROUP, g * K_PASS : (g + 1) * K_PASS].rearrange(
+                    "(r p) k -> p r k", p=P
+                ),
+            )
+            first_bytes.append(t)
+
+        x_flat = x.flatten_outer_dims()
+        x_rows = []
+        for tt in range(TOKEN_TILES):
+            t = work.tile([P, K], BF16, name="x_rows", tag="rows", bufs=8)
+            nc.sync.dma_start(out=t[:], in_=x_flat[tt * P : (tt + 1) * P, :])
+            x_rows.append(t)
+
+        trig = const.tile([P, 2, 2, HALF], BF16, name="trig")
+        nc.sync.dma_start(out=trig[:, 0, :, :], in_=cos.rearrange("(th p) j -> p th j", p=P))
+        nc.sync.dma_start(out=trig[:, 1, :, :], in_=sin.rearrange("(th p) j -> p th j", p=P))
+        q_bytes = {}
+        k_rows = {}
+        for kind, hg in LOAD_ORDER:
+            for r in range(hg * GROUP_HEADS, (hg + 1) * GROUP_HEADS):
+                if kind == "q":
+                    q_bytes[r] = raw.tile([P, K], U8, name="q_bytes%d" % r)
+                    nc.sync.dma_start(out=q_bytes[r][:], in_=Wq_bytes[r * P : (r + 1) * P, :])
+                else:
+                    k_rows[r] = raw.tile([P, K], BF16, name="k_rows%d" % r)
+                    nc.sync.dma_start(out=k_rows[r][:], in_=Wk[r * P : (r + 1) * P, :])
+        norm_rows = {}
+        for kind, w in (("q", q_norm_w), ("k", k_norm_w)):
+            norm_rows[kind] = const.tile([P, HEAD], BF16, name="norm_rows_" + kind)
+            nc.sync.dma_start(out=norm_rows[kind][:], in_=w.partition_broadcast(P))
+
+        ident = const.tile([P, P], F32, name="ident")
+        make_identity(nc, ident[:])
+        ident_bf = const.tile([P, P], BF16, name="ident_bf")
+        make_identity(nc, ident_bf[:])
+
+        one = const.tile([P, 1], F32, name="one")
+        nc.vector.memset(one[:], 1.0)
+        warm = const.tile([P, 1], F32, name="warm")
+        nc.scalar.activation(out=warm[:], in_=one[:], func=ACT.Sqrt)
+
+        zeros = const.tile([P, GROUP], BF16, name="zeros")
+        nc.vector.memset(zeros[:], 0.0)
+
+        def keep_warm(count):
+            idle = psum.tile([P, GROUP], F32, name="idle", tag="acc", bufs=3)
+            for j in range(count):
+                nc.tensor.matmul(out=idle[:], lhsT=ident_bf[:], rhs=zeros[:], start=True, stop=True)
+
+        def turn(sources, slots, grouped):
+            bank = psum.tile([P, 2, 2, P], F32, name="turned", tag="turned", bufs=4)
+            for i, (rows, g) in enumerate(sources):
+                words = rows[:].bitcast(F32)
+                for u in range(2):
+                    nc.tensor.transpose(
+                        bank[:, i, u, :], words[:, 256 * g + u : 256 * (g + 1) : 2], ident[:]
+                    )
+            out_words = grouped[:].bitcast(F32).rearrange("p (s r u) -> p s r u", s=4, u=2)
+            nc.scalar.copy(out=out_words[:, slots, :, :], in_=bank[:].rearrange("p s u r -> p s r u"))
+
+        x_codes = const.tile([P, TOKEN_TILES, K_PASS], U32, name="x_codes", align_bytes=64)
+        x_scales = const.tile([P, TOKEN_TILES, K_PASS], U8, name="x_scales", align_bytes=64)
+        x_grouped = {}
+
+        def turn_x(tt):
+            grouped = work.tile([P, K], BF16, name="x_grouped", bufs=2, align_bytes=64)
+            turn([(x_rows[tt], 0), (x_rows[tt], 1)], slice(0, 2), grouped)
+            turn([(x_rows[tt], 2), (x_rows[tt], 3)], slice(2, 4), grouped)
+            x_grouped[tt] = grouped
+
+        def quantise_x(tt):
+            nc.vector.quantize_mx(
+                out=x_codes[:, tt, :].bitcast(FP8X4), scales=x_scales[:, tt, :], in_=x_grouped[tt][:]
+            )
+
+        rows_of = {}
+        for i, (kind, hg) in enumerate(GROUPS):
+            if kind == "k":
+                rows_of[i] = [k_rows[r] for r in range(hg * GROUP_HEADS, (hg + 1) * GROUP_HEADS)]
+            else:
+                rows_of[i] = []
+
+        def widen(out, codes, cols):
+            nc.vector.tensor_tensor(
+                out=out, in0=codes.bitcast(FP8), in1=scale_bc[:, cols], op=ALU.mult
+            )
+
+        def widen_row_tile(i):
+            r = GROUPS[i][1] * GROUP_HEADS + len(rows_of[i])
+            wide = work.tile([P, K], BF16, name="q_rows", tag="rows", bufs=8)
+            widen(wide[:], q_bytes[r][:], slice(0, K))
+            rows_of[i].append(wide)
+
+        codes_of = {}
+        grouped_of = {}
+
+        def turn_pass(i, g):
+            grouped = work.tile([P, K], BF16, name="grouped", bufs=4, align_bytes=64)
+            rows = rows_of[i]
+            turn([(rows[0], g), (rows[1], g)], slice(0, 2), grouped)
+            turn([(rows[2], g), (rows[3], g)], slice(2, 4), grouped)
+            grouped_of[(i, g)] = grouped
+
+        def quantise_pass(i, g):
+            if g == 0:
+                codes = work.tile([P, PASSES, GROUP], U32, name="w_codes", bufs=2, align_bytes=64)
+                scales = work.tile([P, PASSES, GROUP], U8, name="w_scales", bufs=2, align_bytes=64)
+                codes_of[i] = (codes, scales)
+            codes, scales = codes_of[i]
+            nc.vector.quantize_mx(
+                out=codes[:, g, :].bitcast(FP8X4), scales=scales[:, g, :], in_=grouped_of[(i, g)][:]
+            )
+
+        acc_of = {}
+
+        def multiply(i, tt):
+            codes, scales = codes_of[i]
+            acc = psum.tile([P, GROUP], F32, name="acc", tag="acc", bufs=3)
+            for g in range(PASSES):
+                tok = slice(g * P, (g + 1) * P)
+                nc.tensor.matmul_mx(
+                    out=acc[:],
+                    lhsT=x_codes[:, tt, tok].bitcast(FP8X4),
+                    lhsT_scale=x_scales[:, tt, tok],
+                    rhs=codes[:, g, :].bitcast(FP8X4),
+                    rhs_scale=scales[:, g, :],
+                    start=(g == 0),
+                    stop=(g == PASSES - 1),
+                )
+            acc_of[(i, tt)] = acc
+
+        roped_of = {}
+        sumsq_of = {}
+        inv_of = {}
+
+        prod_of = {}
+
+        def rope_products(i, tt):
+            acc = acc_of[(i, tt)]
+            shape = [P, 2, GROUP_HEADS, HEAD]
+            prod = work.tile([P, 2, GROUP], F32, name="prod", bufs=4)
+            nc.vector.tensor_tensor(
+                out=prod[:].rearrange("p w (h d) -> p w h d", d=HEAD),
+                in0=acc[:].rearrange("p (h d) -> p h d", d=HEAD).unsqueeze(1).to_broadcast(shape),
+                in1=rope_tab[tt % 2][:].unsqueeze(2).to_broadcast(shape),
+                op=ALU.mult,
+            )
+            prod_of[(i, tt)] = prod
+
+        def rope_add(i, tt, f, adder):
+            prod = prod_of[(i, tt)]
+            if f == 0:
+                roped_of[(i, tt)] = work.tile([P, GROUP], F32, name="roped", bufs=10)
+            parts = "p (h f j) -> p h f j"
+            same = prod[:, 0, :].rearrange(parts, f=2, j=HALF)
+            cross = prod[:, 1, :].rearrange(parts, f=2, j=HALF)
+            out = roped_of[(i, tt)][:].rearrange(parts, f=2, j=HALF)
+            adder.tensor_tensor(
+                out=out[:, :, f, :], in0=same[:, :, f, :], in1=cross[:, :, 1 - f, :], op=ALU.add
+            )
+
+        def sum_squares(i, tt):
+            roped = roped_of[(i, tt)]
+            if tt == 0:
+                sumsq_of[i] = work.tile([P, TOKEN_TILES * GROUP_HEADS], F32, name="sumsq", bufs=2)
+            for h in range(GROUP_HEADS):
+                squares = work.tile([P, HEAD], BF16, name="squares", bufs=2)
+                col = tt * GROUP_HEADS + h
+                nc.scalar.activation(
+                    out=squares[:],
+                    in_=roped[:, h * HEAD : (h + 1) * HEAD],
+                    func=ACT.Square,
+                    accum_out=sumsq_of[i][:, col : col + 1],
+                )
+
+        def rope_sum(i, tt, adder):
+            rope_add(i, tt, 0, adder)
+            rope_add(i, tt, 1, adder)
+            sum_squares(i, tt)
+
+        def rope(i, tt):
+            rope_products(i, tt)
+            rope_sum(i, tt, nc.gpsimd)
+
+        rms_of = {}
+
+        def root_mean_square(i, tts):
+            if tts[0] == 0:
+                rms_of[i] = work.tile([P, TOKEN_TILES * GROUP_HEADS], F32, name="rms", bufs=2)
+            cols = slice(tts[0] * GROUP_HEADS, (tts[-1] + 1) * GROUP_HEADS)
+            nc.scalar.activation(
+                out=rms_of[i][:, cols], in_=sumsq_of[i][:, cols], func=ACT.Sqrt, bias=EPS, scale=1.0 / HEAD
+            )
+
+        def finish(i, tts, fused=False):
+            kind, hg = GROUPS[i]
+            dst = out_0 if kind == "q" else out_1
+            if tts[0] == 0:
+                inv_of[i] = work.tile([P, TOKEN_TILES * GROUP_HEADS], F32, name="inv", bufs=2)
+            inv = inv_of[i]
+            cols = slice(tts[0] * GROUP_HEADS, (tts[-1] + 1) * GROUP_HEADS)
+            nc.vector.reciprocal(out=inv[:, cols], in_=rms_of[i][:, cols])
+            for tt in tts:
+                roped = roped_of[(i, tt)]
+                by_head = roped[:].rearrange("p (h d) -> p h d", d=HEAD)
+                if not fused:
+                    nc.vector.tensor_tensor(
+                        out=by_head,
+                        in0=by_head,
+                        in1=norm_w[kind].unsqueeze(1).to_broadcast([P, GROUP_HEADS, HEAD]),
+                        op=ALU.mult,
+                    )
+                for h in range(GROUP_HEADS):
+                    cols = slice(h * HEAD, (h + 1) * HEAD)
+                    col = tt * GROUP_HEADS + h
+                    if fused:
+                        nc.vector.scalar_tensor_tensor(
+                            out=roped[:, cols],
+                            in0=roped[:, cols],
+                            scalar=inv[:, col : col + 1],
+                            in1=norm_w[kind],
+                            op0=ALU.mult,
+                            op1=ALU.mult,
+                        )
+                    else:
+                        nc.scalar.activation(
+                            out=roped[:, cols], in_=roped[:, cols], func=ACT.Copy, scale=inv[:, col : col + 1]
+                        )
+                b, th = tt // 2, tt % 2
+                nc.sync.dma_start(
+                    out=dst[
+                        b, hg * GROUP_HEADS : (hg + 1) * GROUP_HEADS, th * P : (th + 1) * P, :
+                    ].rearrange("h t d -> t h d"),
+                    in_=by_head,
+                )
+
+        def park_norm_weights():
+            norm_bank = psum.tile([P, 2, HEAD], F32, name="norm_bank", tag="norm_bank", bufs=1)
+            for i, kind in enumerate(("q", "k")):
+                nc.tensor.matmul(
+                    out=norm_bank[:, i, :], lhsT=ident_bf[:], rhs=norm_rows[kind][:], start=True, stop=True
+                )
+                norm_w[kind] = norm_bank[:, i, :]
+
+        first_rows = [
+            work.tile([P, K], BF16, name="q_rows", tag="rows", bufs=8) for r in range(GROUP_HEADS)
+        ]
+        rows_of[0] = first_rows
+
+        def widen_first(g):
+            cols = slice(g * K_PASS, (g + 1) * K_PASS)
+            for r in range(GROUP_HEADS):
+                widen(first_rows[r][:, cols], first_bytes[g][:, r, :], cols)
+
+        to_widen = [i for i, (kind, hg) in enumerate(GROUPS) if kind == "q" and i > 0 for r in range(4)]
+
+        keep_warm(WARM_START)
+
+        bank = psum.tile([P, 2, 2, P], F32, name="turned", tag="turned", bufs=4)
+        nc.tensor.transpose(bank[:, 0, 0, :], scale_rows[:], ident[:])
+        scale_cols = const.tile([P, K // P], F32, name="scale_cols")
+        nc.scalar.copy(out=scale_cols[:], in_=bank[:, 0, 0, 0 : K // P])
+        scale_bc = const.tile([P, K], F32, name="scale_bc")
+        for g in range(PASSES):
+            bank = psum.tile([P, 4, P], F32, name="turned", tag="turned", bufs=4)
+            for i in range(4):
+                m = 4 * g + i
+                nc.tensor.transpose(bank[:, i, :], scale_cols[:, m : m + 1].to_broadcast([P, P]), ident[:])
+            nc.scalar.copy(
+                out=scale_bc[:, g * K_PASS : (g + 1) * K_PASS], in_=bank[:].rearrange("p i c -> p (i c)")
+            )
+
+        widen_first(0)
+        turn_pass(0, 0)
+        keep_warm(WARM)
+        widen_first(1)
+        turn_pass(0, 1)
+        keep_warm(WARM)
+        turn_x(0)
+        keep_warm(WARM)
+        turn_x(1)
+        keep_warm(WARM)
+        widen_first(2)
+        turn_pass(0, 2)
+        keep_warm(WARM)
+        widen_first(3)
+        turn_pass(0, 3)
+        keep_warm(WARM)
+        quantise_pass(0, 0)
+        quantise_pass(0, 1)
+        quantise_x(0)
+        turn_x(2)
+        keep_warm(WARM)
+        widen_row_tile(to_widen[0])
+        quantise_x(1)
+        turn_x(3)
+        keep_warm(WARM)
+        quantise_pass(0, 2)
+        widen_row_tile(to_widen[1])
+        quantise_pass(0, 3)
+        quantise_x(2)
+        quantise_x(3)
+        for g in range(PASSES):
+            turn_pass(1, g)
+            keep_warm(WARM)
+        multiply(0, 0)
+        multiply(0, 1)
+        multiply(0, 2)
+
+        for j in range(2, FILL[0]):
+            widen_row_tile(to_widen[j])
+
+        rope_tab = []
+        for th in range(2):
+            t = const.tile([P, 2, HEAD], BF16, name="rope_tab%d" % th)
+            nc.scalar.copy(out=t[:, 0, 0:HALF], in_=trig[:, 0, th, :])
+            nc.scalar.copy(out=t[:, 0, HALF:HEAD], in_=trig[:, 0, th, :])
+            nc.scalar.copy(out=t[:, 1, 0:HALF], in_=trig[:, 1, th, :])
+            nc.scalar.activation(out=t[:, 1, HALF:HEAD], in_=trig[:, 1, th, :], func=ACT.Copy, scale=-1.0)
+            rope_tab.append(t)
+
+        all_tiles = list(range(TOKEN_TILES))
+        last = n_groups - 1
+        norm_w = {}
+        for n in range(last):
+            for g in range(PASSES):
+                quantise_pass(n + 1, g)
+            if n == 1:
+                park_norm_weights()
+            if n + 2 < n_groups:
+                turn_pass(n + 2, 0)
+                turn_pass(n + 2, 1)
+            rope(n, 0)
+            multiply(n, 3)
+            rope(n, 1)
+            multiply(n + 1, 0)
+            if n + 2 < n_groups:
+                turn_pass(n + 2, 2)
+                turn_pass(n + 2, 3)
+            if n > 0:
+                rope(n, 2)
+                multiply(n + 1, 1)
+                finish(n - 1, [0, 1])
+                rope(n, 3)
+                multiply(n + 1, 2)
+                root_mean_square(n, all_tiles)
+                finish(n - 1, [2, 3])
+            else:
+                rope_products(n, 2)
+                multiply(n + 1, 1)
+                rope_products(n, 3)
+                multiply(n + 1, 2)
+                rope_sum(n, 2, nc.vector)
+                rope_sum(n, 3, nc.vector)
+                root_mean_square(n, all_tiles)
+            for j in range(FILL[n], FILL[n + 1]):
+                widen_row_tile(to_widen[j])
+
+        rope_products(last, 0)
+        multiply(last, 3)
+        rope_products(last, 1)
+        rope_sum(last, 0, nc.vector)
+        root_mean_square(last, [0])
+        rope_sum(last, 1, nc.vector)
+        root_mean_square(last, [1])
+        finish(last - 1, all_tiles)
+        rope_products(last, 2)
+        rope_products(last, 3)
+        rope_sum(last, 2, nc.vector)
+        root_mean_square(last, [2])
+        rope_sum(last, 3, nc.vector)
+        root_mean_square(last, [3])
+        finish(last, [0, 1], fused=True)
+        finish(last, [2, 3], fused=True)

@@ -21,22 +21,25 @@ PASSES = K // K_PASS
 TOKEN_TILES = 4
 HEAD = 128
 HALF = HEAD // 2
-GROUP_HEADS = 4
-GROUP = GROUP_HEADS * HEAD
+PAIR = 2
+GROUP = 2 * PAIR * HEAD
+N_GROUPS = 8
+N_PASSES = N_GROUPS * PASSES
+N_TILES = N_GROUPS * TOKEN_TILES
 EPS = 2.0 ** -23
-FILL = [6, 7, 8, 9, 10, 12, 12, 12, 12]
-WARM_START = 4
-WARM = 2
 
-GROUPS = [("q", 0), ("k", 0), ("k", 1), ("q", 1), ("k", 2), ("q", 2), ("k", 3), ("q", 3)]
-LOAD_ORDER = [("q", 1), ("k", 0), ("k", 1), ("q", 2), ("k", 2), ("q", 3), ("k", 3)]
+X_ON_SCALAR = (0, 1, 2, 3)
+FUSED_TILES = (2, 3)
+
+
+def fused_on_vector(ti):
+    return ti % 4 in FUSED_TILES or ti >= N_TILES - 4
 
 
 def tile_attention_pa_kernel(
     tc, x, sin, cos, Wq_bytes, Wq_scale, Wk, q_norm_w, k_norm_w, out_0, out_1
 ):
     nc = tc.nc
-    n_groups = len(GROUPS)
 
     with ExitStack() as ctx:
         const = ctx.enter_context(tc.tile_pool(name="const", bufs=1))
@@ -45,47 +48,50 @@ def tile_attention_pa_kernel(
         psum = ctx.enter_context(tc.psum_pool(name="psum", bufs=1))
         ctx.enter_context(tc.manual_schedule())
 
-        scale_rows = const.tile([P, P], F32, name="scale_rows")
-        nc.vector.memset(scale_rows[:], 0.0)
-        nc.scalar.dma_start(
-            out=scale_rows[0 : K // P, :], in_=Wq_scale.rearrange("o (m p) -> (o m) p", p=P)
-        )
+        k_scale = const.tile([P, PASSES, 4], F32, name="k_scale")
+        nc.scalar.dma_start(out=k_scale[:], in_=Wq_scale.rearrange("o (g p t) -> p (o g) t", p=P, t=4))
 
-        first_bytes = []
-        for g in range(PASSES):
-            t = raw.tile([P, GROUP_HEADS, K_PASS], U8, name="first_bytes%d" % g)
-            nc.sync.dma_start(
-                out=t[:],
-                in_=Wq_bytes[0:GROUP, g * K_PASS : (g + 1) * K_PASS].rearrange(
-                    "(r p) k -> p r k", p=P
-                ),
-            )
-            first_bytes.append(t)
-
+        q_bytes = {}
+        k_rows = {}
         x_flat = x.flatten_outer_dims()
         x_rows = []
-        for tt in range(TOKEN_TILES):
-            t = work.tile([P, K], BF16, name="x_rows", tag="rows", bufs=8)
+
+        def load_group(i):
+            rows = slice(i * PAIR * P, (i + 1) * PAIR * P)
+            q_bytes[i] = raw.tile([P, PAIR, K], U8, name="q_bytes%d" % i)
+            nc.sync.dma_start(out=q_bytes[i][:], in_=Wq_bytes[rows, :].rearrange("(r p) k -> p r k", p=P))
+            k_rows[i] = raw.tile([P, PAIR, K], BF16, name="k_rows%d" % i)
+            nc.sync.dma_start(out=k_rows[i][:], in_=Wk[rows, :].rearrange("(r p) k -> p r k", p=P))
+
+        def load_x(tt):
+            t = work.tile([P, K], BF16, name="x_rows", tag="rows", bufs=6)
             nc.sync.dma_start(out=t[:], in_=x_flat[tt * P : (tt + 1) * P, :])
             x_rows.append(t)
 
+        q_bytes[0] = raw.tile([P, PAIR, K], U8, name="q_bytes0")
+        k_rows[0] = raw.tile([P, PAIR, K], BF16, name="k_rows0")
+        first = slice(0, PAIR * P)
+
+        def load_first(tile, src, half):
+            cols = slice(half * K // 2, (half + 1) * K // 2)
+            nc.sync.dma_start(out=tile[:, :, cols], in_=src[first, cols].rearrange("(r p) k -> p r k", p=P))
+
         trig = const.tile([P, 2, 2, HALF], BF16, name="trig")
+        norm_rows = const.tile([P, 2, HEAD], BF16, name="norm_rows")
+        load_first(q_bytes[0], Wq_bytes, 0)
+        load_first(q_bytes[0], Wq_bytes, 1)
+        load_first(k_rows[0], Wk, 0)
+        load_x(0)
         nc.sync.dma_start(out=trig[:, 0, :, :], in_=cos.rearrange("(th p) j -> p th j", p=P))
         nc.sync.dma_start(out=trig[:, 1, :, :], in_=sin.rearrange("(th p) j -> p th j", p=P))
-        q_bytes = {}
-        k_rows = {}
-        for kind, hg in LOAD_ORDER:
-            for r in range(hg * GROUP_HEADS, (hg + 1) * GROUP_HEADS):
-                if kind == "q":
-                    q_bytes[r] = raw.tile([P, K], U8, name="q_bytes%d" % r)
-                    nc.sync.dma_start(out=q_bytes[r][:], in_=Wq_bytes[r * P : (r + 1) * P, :])
-                else:
-                    k_rows[r] = raw.tile([P, K], BF16, name="k_rows%d" % r)
-                    nc.sync.dma_start(out=k_rows[r][:], in_=Wk[r * P : (r + 1) * P, :])
-        norm_rows = {}
-        for kind, w in (("q", q_norm_w), ("k", k_norm_w)):
-            norm_rows[kind] = const.tile([P, HEAD], BF16, name="norm_rows_" + kind)
-            nc.sync.dma_start(out=norm_rows[kind][:], in_=w.partition_broadcast(P))
+        load_first(k_rows[0], Wk, 1)
+        load_x(1)
+        nc.sync.dma_start(out=norm_rows[:, 0, :], in_=q_norm_w.partition_broadcast(P))
+        nc.sync.dma_start(out=norm_rows[:, 1, :], in_=k_norm_w.partition_broadcast(P))
+        load_x(2)
+        load_x(3)
+        for i in range(1, N_GROUPS):
+            load_group(i)
 
         ident = const.tile([P, P], F32, name="ident")
         make_identity(nc, ident[:])
@@ -97,33 +103,38 @@ def tile_attention_pa_kernel(
         warm = const.tile([P, 1], F32, name="warm")
         nc.scalar.activation(out=warm[:], in_=one[:], func=ACT.Sqrt)
 
-        zeros = const.tile([P, GROUP], BF16, name="zeros")
-        nc.vector.memset(zeros[:], 0.0)
-
-        def keep_warm(count):
-            idle = psum.tile([P, GROUP], F32, name="idle", tag="acc", bufs=3)
-            for j in range(count):
-                nc.tensor.matmul(out=idle[:], lhsT=ident_bf[:], rhs=zeros[:], start=True, stop=True)
-
-        def turn(sources, slots, grouped):
+        def turn(sources):
             bank = psum.tile([P, 2, 2, P], F32, name="turned", tag="turned", bufs=4)
-            for i, (rows, g) in enumerate(sources):
-                words = rows[:].bitcast(F32)
+            for s, (rows, g) in enumerate(sources):
+                words = rows.bitcast(F32)
                 for u in range(2):
-                    nc.tensor.transpose(
-                        bank[:, i, u, :], words[:, 256 * g + u : 256 * (g + 1) : 2], ident[:]
-                    )
-            out_words = grouped[:].bitcast(F32).rearrange("p (s r u) -> p s r u", s=4, u=2)
-            nc.scalar.copy(out=out_words[:, slots, :, :], in_=bank[:].rearrange("p s u r -> p s r u"))
+                    nc.tensor.transpose(bank[:, u, s, :], words[:, 256 * g + u : 256 * (g + 1) : 2], ident[:])
+            return bank
+
+        def copy_out(engine_copy, bank, grouped, half):
+            out_words = grouped[:, half * 1024 : (half + 1) * 1024].bitcast(F32)
+            engine_copy(
+                out=out_words.rearrange("p (c u) -> p c u", u=2), in_=bank[:].rearrange("p u s r -> p (s r) u")
+            )
+
+        def scale_out(bank, grouped, g):
+            shape = [P, 2 * P, 2, 2]
+            nc.vector.tensor_tensor(
+                out=grouped[:, 0:1024].rearrange("p (c u e) -> p c u e", u=2, e=2),
+                in0=bank[:].bitcast(BF16).rearrange("p u s (r e) -> p (s r) u e", e=2),
+                in1=k_scale[:, g, :].rearrange("p (u e) -> p u e", e=2).unsqueeze(1).to_broadcast(shape),
+                op=ALU.mult,
+            )
 
         x_codes = const.tile([P, TOKEN_TILES, K_PASS], U32, name="x_codes", align_bytes=64)
         x_scales = const.tile([P, TOKEN_TILES, K_PASS], U8, name="x_scales", align_bytes=64)
         x_grouped = {}
 
         def turn_x(tt):
-            grouped = work.tile([P, K], BF16, name="x_grouped", bufs=2, align_bytes=64)
-            turn([(x_rows[tt], 0), (x_rows[tt], 1)], slice(0, 2), grouped)
-            turn([(x_rows[tt], 2), (x_rows[tt], 3)], slice(2, 4), grouped)
+            grouped = work.tile([P, K], BF16, name="x_grouped", tag="grouped", bufs=5, align_bytes=64)
+            rows = x_rows[tt][:]
+            copy_out(nc.scalar.copy, turn([(rows, 0), (rows, 1)]), grouped, 0)
+            copy_out(nc.scalar.copy if tt in X_ON_SCALAR else nc.vector.tensor_copy, turn([(rows, 2), (rows, 3)]), grouped, 1)
             x_grouped[tt] = grouped
 
         def quantise_x(tt):
@@ -131,47 +142,57 @@ def tile_attention_pa_kernel(
                 out=x_codes[:, tt, :].bitcast(FP8X4), scales=x_scales[:, tt, :], in_=x_grouped[tt][:]
             )
 
-        rows_of = {}
-        for i, (kind, hg) in enumerate(GROUPS):
-            if kind == "k":
-                rows_of[i] = [k_rows[r] for r in range(hg * GROUP_HEADS, (hg + 1) * GROUP_HEADS)]
-            else:
-                rows_of[i] = []
+        q_wide = {}
 
-        def widen(out, codes, cols):
-            nc.vector.tensor_tensor(
-                out=out, in0=codes.bitcast(FP8), in1=scale_bc[:, cols], op=ALU.mult
-            )
+        def cast(copy, ci, part, parts):
+            i, r = ci // PAIR, ci % PAIR
+            if ci not in q_wide:
+                q_wide[ci] = work.tile([P, K], BF16, name="q_wide", tag="rows", bufs=6)
+            cols = slice(part * K // parts, (part + 1) * K // parts)
+            copy(out=q_wide[ci][:, cols], in_=q_bytes[i][:, r, cols].bitcast(FP8))
 
-        def widen_row_tile(i):
-            r = GROUPS[i][1] * GROUP_HEADS + len(rows_of[i])
-            wide = work.tile([P, K], BF16, name="q_rows", tag="rows", bufs=8)
-            widen(wide[:], q_bytes[r][:], slice(0, K))
-            rows_of[i].append(wide)
+        def cast_half(hi):
+            i, j = hi // 4, hi % 4
+            cast(nc.scalar.copy, PAIR * i + j % 2, j // 2, 2)
 
-        codes_of = {}
         grouped_of = {}
+        banks_of = {}
+        codes_of = {}
 
-        def turn_pass(i, g):
-            grouped = work.tile([P, K], BF16, name="grouped", bufs=4, align_bytes=64)
-            rows = rows_of[i]
-            turn([(rows[0], g), (rows[1], g)], slice(0, 2), grouped)
-            turn([(rows[2], g), (rows[3], g)], slice(2, 4), grouped)
-            grouped_of[(i, g)] = grouped
+        def turn_q(pi):
+            i, g = pi // PASSES, pi % PASSES
+            grouped_of[pi] = work.tile([P, K], BF16, name="grouped", tag="grouped", bufs=5, align_bytes=64)
+            banks_of[pi] = [turn([(q_wide[PAIR * i][:], g), (q_wide[PAIR * i + 1][:], g)])]
 
-        def quantise_pass(i, g):
+        def turn_k(pi):
+            i, g = pi // PASSES, pi % PASSES
+            banks_of[pi].append(turn([(k_rows[i][:, 0, :], g), (k_rows[i][:, 1, :], g)]))
+
+        def turn_pass(pi):
+            turn_q(pi)
+            turn_k(pi)
+
+        def empty_q(pi):
+            scale_out(banks_of[pi][0], grouped_of[pi], pi % PASSES)
+
+        def empty_k(pi):
+            copy_out(nc.scalar.copy, banks_of[pi][1], grouped_of[pi], 1)
+
+        def quantise_pass(pi):
+            i, g = pi // PASSES, pi % PASSES
             if g == 0:
-                codes = work.tile([P, PASSES, GROUP], U32, name="w_codes", bufs=2, align_bytes=64)
-                scales = work.tile([P, PASSES, GROUP], U8, name="w_scales", bufs=2, align_bytes=64)
+                codes = work.tile([P, PASSES, GROUP], U32, name="w_codes", bufs=3, align_bytes=64)
+                scales = work.tile([P, PASSES, GROUP], U8, name="w_scales", bufs=3, align_bytes=64)
                 codes_of[i] = (codes, scales)
             codes, scales = codes_of[i]
             nc.vector.quantize_mx(
-                out=codes[:, g, :].bitcast(FP8X4), scales=scales[:, g, :], in_=grouped_of[(i, g)][:]
+                out=codes[:, g, :].bitcast(FP8X4), scales=scales[:, g, :], in_=grouped_of[pi][:]
             )
 
         acc_of = {}
 
-        def multiply(i, tt):
+        def multiply(ti):
+            i, tt = ti // TOKEN_TILES, ti % TOKEN_TILES
             codes, scales = codes_of[i]
             acc = psum.tile([P, GROUP], F32, name="acc", tag="acc", bufs=3)
             for g in range(PASSES):
@@ -185,248 +206,235 @@ def tile_attention_pa_kernel(
                     start=(g == 0),
                     stop=(g == PASSES - 1),
                 )
-            acc_of[(i, tt)] = acc
-
-        roped_of = {}
-        sumsq_of = {}
-        inv_of = {}
+            acc_of[ti] = acc
 
         prod_of = {}
+        roped_of = {}
+        sumsq_of = {}
+        rms_of = {}
+        inv_of = {}
 
-        def rope_products(i, tt):
-            acc = acc_of[(i, tt)]
-            shape = [P, 2, GROUP_HEADS, HEAD]
+        def rope_products(ti):
+            shape = [P, 2, 2 * PAIR, HEAD]
             prod = work.tile([P, 2, GROUP], F32, name="prod", bufs=4)
             nc.vector.tensor_tensor(
                 out=prod[:].rearrange("p w (h d) -> p w h d", d=HEAD),
-                in0=acc[:].rearrange("p (h d) -> p h d", d=HEAD).unsqueeze(1).to_broadcast(shape),
-                in1=rope_tab[tt % 2][:].unsqueeze(2).to_broadcast(shape),
+                in0=acc_of[ti][:].rearrange("p (h d) -> p h d", d=HEAD).unsqueeze(1).to_broadcast(shape),
+                in1=rope_tab[ti % 2][:].unsqueeze(2).to_broadcast(shape),
                 op=ALU.mult,
             )
-            prod_of[(i, tt)] = prod
+            prod_of[ti] = prod
 
-        def rope_add(i, tt, f, adder):
-            prod = prod_of[(i, tt)]
-            if f == 0:
-                roped_of[(i, tt)] = work.tile([P, GROUP], F32, name="roped", bufs=10)
+        def rope_add(ti, adder):
+            prod = prod_of[ti]
+            roped_of[ti] = work.tile([P, GROUP], F32, name="roped", bufs=12)
             parts = "p (h f j) -> p h f j"
             same = prod[:, 0, :].rearrange(parts, f=2, j=HALF)
             cross = prod[:, 1, :].rearrange(parts, f=2, j=HALF)
-            out = roped_of[(i, tt)][:].rearrange(parts, f=2, j=HALF)
-            adder.tensor_tensor(
-                out=out[:, :, f, :], in0=same[:, :, f, :], in1=cross[:, :, 1 - f, :], op=ALU.add
-            )
+            out = roped_of[ti][:].rearrange(parts, f=2, j=HALF)
+            for f in range(2):
+                adder.tensor_tensor(
+                    out=out[:, :, f, :], in0=same[:, :, f, :], in1=cross[:, :, 1 - f, :], op=ALU.add
+                )
 
-        def sum_squares(i, tt):
-            roped = roped_of[(i, tt)]
+        def sum_squares(ti):
+            i, tt = ti // TOKEN_TILES, ti % TOKEN_TILES
             if tt == 0:
-                sumsq_of[i] = work.tile([P, TOKEN_TILES * GROUP_HEADS], F32, name="sumsq", bufs=2)
-            for h in range(GROUP_HEADS):
+                sumsq_of[i] = work.tile([P, 4 * TOKEN_TILES], F32, name="sumsq", bufs=3)
+                rms_of[i] = work.tile([P, 4 * TOKEN_TILES], F32, name="rms", bufs=3)
+                inv_of[i] = work.tile([P, 4 * TOKEN_TILES], F32, name="inv", bufs=3)
+            for h in range(2 * PAIR):
                 squares = work.tile([P, HEAD], BF16, name="squares", bufs=2)
-                col = tt * GROUP_HEADS + h
+                col = tt * 4 + h
                 nc.scalar.activation(
                     out=squares[:],
-                    in_=roped[:, h * HEAD : (h + 1) * HEAD],
+                    in_=roped_of[ti][:, h * HEAD : (h + 1) * HEAD],
                     func=ACT.Square,
                     accum_out=sumsq_of[i][:, col : col + 1],
                 )
 
-        def rope_sum(i, tt, adder):
-            rope_add(i, tt, 0, adder)
-            rope_add(i, tt, 1, adder)
-            sum_squares(i, tt)
-
-        def rope(i, tt):
-            rope_products(i, tt)
-            rope_sum(i, tt, nc.gpsimd)
-
-        rms_of = {}
-
         def root_mean_square(i, tts):
-            if tts[0] == 0:
-                rms_of[i] = work.tile([P, TOKEN_TILES * GROUP_HEADS], F32, name="rms", bufs=2)
-            cols = slice(tts[0] * GROUP_HEADS, (tts[-1] + 1) * GROUP_HEADS)
+            cols = slice(tts[0] * 4, (tts[-1] + 1) * 4)
             nc.scalar.activation(
                 out=rms_of[i][:, cols], in_=sumsq_of[i][:, cols], func=ACT.Sqrt, bias=EPS, scale=1.0 / HEAD
             )
 
-        def finish(i, tts, fused=False):
-            kind, hg = GROUPS[i]
-            dst = out_0 if kind == "q" else out_1
-            if tts[0] == 0:
-                inv_of[i] = work.tile([P, TOKEN_TILES * GROUP_HEADS], F32, name="inv", bufs=2)
-            inv = inv_of[i]
-            cols = slice(tts[0] * GROUP_HEADS, (tts[-1] + 1) * GROUP_HEADS)
-            nc.vector.reciprocal(out=inv[:, cols], in_=rms_of[i][:, cols])
-            for tt in tts:
-                roped = roped_of[(i, tt)]
-                by_head = roped[:].rearrange("p (h d) -> p h d", d=HEAD)
-                if not fused:
-                    nc.vector.tensor_tensor(
-                        out=by_head,
-                        in0=by_head,
-                        in1=norm_w[kind].unsqueeze(1).to_broadcast([P, GROUP_HEADS, HEAD]),
-                        op=ALU.mult,
-                    )
-                for h in range(GROUP_HEADS):
-                    cols = slice(h * HEAD, (h + 1) * HEAD)
-                    col = tt * GROUP_HEADS + h
-                    if fused:
-                        nc.vector.scalar_tensor_tensor(
-                            out=roped[:, cols],
-                            in0=roped[:, cols],
-                            scalar=inv[:, col : col + 1],
-                            in1=norm_w[kind],
-                            op0=ALU.mult,
-                            op1=ALU.mult,
-                        )
-                    else:
-                        nc.scalar.activation(
-                            out=roped[:, cols], in_=roped[:, cols], func=ACT.Copy, scale=inv[:, col : col + 1]
-                        )
-                b, th = tt // 2, tt % 2
-                nc.sync.dma_start(
-                    out=dst[
-                        b, hg * GROUP_HEADS : (hg + 1) * GROUP_HEADS, th * P : (th + 1) * P, :
-                    ].rearrange("h t d -> t h d"),
-                    in_=by_head,
-                )
+        def invert(i, tts):
+            cols = slice(tts[0] * 4, (tts[-1] + 1) * 4)
+            nc.vector.reciprocal(out=inv_of[i][:, cols], in_=rms_of[i][:, cols])
 
-        def park_norm_weights():
-            norm_bank = psum.tile([P, 2, HEAD], F32, name="norm_bank", tag="norm_bank", bufs=1)
-            for i, kind in enumerate(("q", "k")):
-                nc.tensor.matmul(
-                    out=norm_bank[:, i, :], lhsT=ident_bf[:], rhs=norm_rows[kind][:], start=True, stop=True
-                )
-                norm_w[kind] = norm_bank[:, i, :]
-
-        first_rows = [
-            work.tile([P, K], BF16, name="q_rows", tag="rows", bufs=8) for r in range(GROUP_HEADS)
-        ]
-        rows_of[0] = first_rows
-
-        def widen_first(g):
-            cols = slice(g * K_PASS, (g + 1) * K_PASS)
-            for r in range(GROUP_HEADS):
-                widen(first_rows[r][:, cols], first_bytes[g][:, r, :], cols)
-
-        to_widen = [i for i, (kind, hg) in enumerate(GROUPS) if kind == "q" and i > 0 for r in range(4)]
-
-        keep_warm(WARM_START)
-
-        bank = psum.tile([P, 2, 2, P], F32, name="turned", tag="turned", bufs=4)
-        nc.tensor.transpose(bank[:, 0, 0, :], scale_rows[:], ident[:])
-        scale_cols = const.tile([P, K // P], F32, name="scale_cols")
-        nc.scalar.copy(out=scale_cols[:], in_=bank[:, 0, 0, 0 : K // P])
-        scale_bc = const.tile([P, K], F32, name="scale_bc")
-        for g in range(PASSES):
-            bank = psum.tile([P, 4, P], F32, name="turned", tag="turned", bufs=4)
-            for i in range(4):
-                m = 4 * g + i
-                nc.tensor.transpose(bank[:, i, :], scale_cols[:, m : m + 1].to_broadcast([P, P]), ident[:])
-            nc.scalar.copy(
-                out=scale_bc[:, g * K_PASS : (g + 1) * K_PASS], in_=bank[:].rearrange("p i c -> p (i c)")
+        def weigh(ti):
+            nc.gpsimd.tensor_tensor(
+                out=roped_of[ti][:].rearrange("p (m h d) -> p m h d", m=2, d=HEAD),
+                in0=roped_of[ti][:].rearrange("p (m h d) -> p m h d", m=2, d=HEAD),
+                in1=norm_rows[:].unsqueeze(2).to_broadcast([P, 2, PAIR, HEAD]),
+                op=ALU.mult,
             )
 
-        widen_first(0)
-        turn_pass(0, 0)
-        keep_warm(WARM)
-        widen_first(1)
-        turn_pass(0, 1)
-        keep_warm(WARM)
-        turn_x(0)
-        keep_warm(WARM)
-        turn_x(1)
-        keep_warm(WARM)
-        widen_first(2)
-        turn_pass(0, 2)
-        keep_warm(WARM)
-        widen_first(3)
-        turn_pass(0, 3)
-        keep_warm(WARM)
-        quantise_pass(0, 0)
-        quantise_pass(0, 1)
-        quantise_x(0)
-        turn_x(2)
-        keep_warm(WARM)
-        widen_row_tile(to_widen[0])
-        quantise_x(1)
-        turn_x(3)
-        keep_warm(WARM)
-        quantise_pass(0, 2)
-        widen_row_tile(to_widen[1])
-        quantise_pass(0, 3)
-        quantise_x(2)
-        quantise_x(3)
-        for g in range(PASSES):
-            turn_pass(1, g)
-            keep_warm(WARM)
-        multiply(0, 0)
-        multiply(0, 1)
-        multiply(0, 2)
+        def store(ti):
+            i, tt = ti // TOKEN_TILES, ti % TOKEN_TILES
+            b, th = tt // 2, tt % 2
+            for m, dst in enumerate((out_0, out_1)):
+                nc.sync.dma_start(
+                    out=dst[b, i * PAIR : (i + 1) * PAIR, th * P : (th + 1) * P, :].rearrange("h t d -> t h d"),
+                    in_=roped_of[ti][:, m * PAIR * HEAD : (m + 1) * PAIR * HEAD].rearrange("p (h d) -> p h d", d=HEAD),
+                )
 
-        for j in range(2, FILL[0]):
-            widen_row_tile(to_widen[j])
+        def normalise(ti, fused):
+            i, tt = ti // TOKEN_TILES, ti % TOKEN_TILES
+            roped = roped_of[ti]
+            for h in range(2 * PAIR):
+                cols = slice(h * HEAD, (h + 1) * HEAD)
+                inv = inv_of[i][:, tt * 4 + h : tt * 4 + h + 1]
+                if fused:
+                    nc.vector.scalar_tensor_tensor(
+                        out=roped[:, cols], in0=roped[:, cols], scalar=inv, in1=norm_bank[:, h // PAIR, :],
+                        op0=ALU.mult, op1=ALU.mult,
+                    )
+                else:
+                    nc.scalar.activation(out=roped[:, cols], in_=roped[:, cols], func=ACT.Copy, scale=inv)
+
+        def make_tables():
+            for th in range(2):
+                t = const.tile([P, 2, HEAD], BF16, name="rope_tab%d" % th)
+                nc.gpsimd.tensor_copy(out=t[:, 0, 0:HALF], in_=trig[:, 0, th, :])
+                nc.gpsimd.tensor_copy(out=t[:, 0, HALF:HEAD], in_=trig[:, 0, th, :])
+                nc.gpsimd.tensor_copy(out=t[:, 1, 0:HALF], in_=trig[:, 1, th, :])
+                nc.gpsimd.tensor_scalar(
+                    out=t[:, 1, HALF:HEAD], in0=trig[:, 1, th, :], scalar1=-1.0, scalar2=0.0, op0=ALU.mult, op1=ALU.add
+                )
+                rope_tab.append(t)
+
+        def park_norm_weights():
+            for m in range(2):
+                nc.tensor.matmul(
+                    out=norm_bank[:, m, :], lhsT=ident_bf[:], rhs=norm_rows[:, m, :], start=True, stop=True
+                )
 
         rope_tab = []
-        for th in range(2):
-            t = const.tile([P, 2, HEAD], BF16, name="rope_tab%d" % th)
-            nc.scalar.copy(out=t[:, 0, 0:HALF], in_=trig[:, 0, th, :])
-            nc.scalar.copy(out=t[:, 0, HALF:HEAD], in_=trig[:, 0, th, :])
-            nc.scalar.copy(out=t[:, 1, 0:HALF], in_=trig[:, 1, th, :])
-            nc.scalar.activation(out=t[:, 1, HALF:HEAD], in_=trig[:, 1, th, :], func=ACT.Copy, scale=-1.0)
-            rope_tab.append(t)
-
+        norm_bank = psum.tile([P, 2, HEAD], F32, name="norm_bank", tag="norm_bank", bufs=1)
         all_tiles = list(range(TOKEN_TILES))
-        last = n_groups - 1
-        norm_w = {}
-        for n in range(last):
-            for g in range(PASSES):
-                quantise_pass(n + 1, g)
-            if n == 1:
-                park_norm_weights()
-            if n + 2 < n_groups:
-                turn_pass(n + 2, 0)
-                turn_pass(n + 2, 1)
-            rope(n, 0)
-            multiply(n, 3)
-            rope(n, 1)
-            multiply(n + 1, 0)
-            if n + 2 < n_groups:
-                turn_pass(n + 2, 2)
-                turn_pass(n + 2, 3)
-            if n > 0:
-                rope(n, 2)
-                multiply(n + 1, 1)
-                finish(n - 1, [0, 1])
-                rope(n, 3)
-                multiply(n + 1, 2)
-                root_mean_square(n, all_tiles)
-                finish(n - 1, [2, 3])
-            else:
-                rope_products(n, 2)
-                multiply(n + 1, 1)
-                rope_products(n, 3)
-                multiply(n + 1, 2)
-                rope_sum(n, 2, nc.vector)
-                rope_sum(n, 3, nc.vector)
-                root_mean_square(n, all_tiles)
-            for j in range(FILL[n], FILL[n + 1]):
-                widen_row_tile(to_widen[j])
 
-        rope_products(last, 0)
-        multiply(last, 3)
-        rope_products(last, 1)
-        rope_sum(last, 0, nc.vector)
-        root_mean_square(last, [0])
-        rope_sum(last, 1, nc.vector)
-        root_mean_square(last, [1])
-        finish(last - 1, all_tiles)
-        rope_products(last, 2)
-        rope_products(last, 3)
-        rope_sum(last, 2, nc.vector)
-        root_mean_square(last, [2])
-        rope_sum(last, 3, nc.vector)
-        root_mean_square(last, [3])
-        finish(last, [0, 1], fused=True)
-        finish(last, [2, 3], fused=True)
+        for g in range(2):
+            for r in range(PAIR):
+                cast(nc.vector.tensor_copy, r, g, PASSES)
+        for g in range(2, PASSES):
+            for r in range(PAIR):
+                cast(nc.scalar.copy, r, g, PASSES)
+        make_tables()
+        turn_q(0)
+        turn_q(1)
+        empty_q(0)
+        turn_k(0)
+        empty_q(1)
+        turn_k(1)
+        empty_k(0)
+        turn_q(2)
+        empty_k(1)
+        turn_q(3)
+        empty_q(2)
+        empty_q(3)
+        turn_x(0)
+        turn_k(2)
+        turn_k(3)
+        empty_k(2)
+        empty_k(3)
+        quantise_x(0)
+        turn_x(1)
+        turn_x(2)
+
+        for n in range(N_GROUPS):
+            t0 = n * TOKEN_TILES
+            nxt = (n + 1) * PASSES if n + 1 < N_GROUPS else None
+            halves = [4 * (n + 2) + h for h in range(4)] if n + 2 < N_GROUPS else []
+            last = n == N_GROUPS - 1
+            for g in range(PASSES):
+                quantise_pass(n * PASSES + g)
+            if n == 0:
+                turn_x(3)
+            multiply(t0)
+            if n == 0:
+                quantise_x(1)
+                quantise_x(2)
+                quantise_x(3)
+                cast_half(4)
+                cast_half(5)
+            multiply(t0 + 1)
+            multiply(t0 + 2)
+            if n == 0:
+                park_norm_weights()
+                turn_pass(4)
+                cast_half(6)
+                cast_half(7)
+                turn_pass(5)
+            if n > 0:
+                invert(n - 1, all_tiles)
+                for tt in all_tiles:
+                    if fused_on_vector(t0 - 4 + tt):
+                        normalise(t0 - 4 + tt, True)
+                        store(t0 - 4 + tt)
+                for tt in all_tiles:
+                    if not fused_on_vector(t0 - 4 + tt):
+                        normalise(t0 - 4 + tt, False)
+                        weigh(t0 - 4 + tt)
+                        store(t0 - 4 + tt)
+            if last:
+                continue
+            if halves:
+                cast_half(halves[0])
+            rope_products(t0)
+            multiply(t0 + 3)
+            rope_products(t0 + 1)
+            rope_add(t0, nc.gpsimd)
+            empty_q(nxt)
+            empty_k(nxt)
+            turn_pass(nxt + 2)
+            rope_add(t0 + 1, nc.gpsimd)
+            rope_products(t0 + 2)
+            if halves:
+                cast_half(halves[1])
+            empty_q(nxt + 1)
+            empty_k(nxt + 1)
+            turn_pass(nxt + 3)
+            sum_squares(t0)
+            rope_add(t0 + 2, nc.gpsimd)
+            rope_products(t0 + 3)
+            empty_q(nxt + 2)
+            empty_k(nxt + 2)
+            sum_squares(t0 + 1)
+            rope_add(t0 + 3, nc.gpsimd)
+            empty_q(nxt + 3)
+            empty_k(nxt + 3)
+            sum_squares(t0 + 2)
+            sum_squares(t0 + 3)
+            root_mean_square(n, all_tiles)
+            if halves:
+                cast_half(halves[2])
+                cast_half(halves[3])
+            if n + 2 < N_GROUPS:
+                turn_pass(nxt + 4)
+                turn_pass(nxt + 5)
+
+        n = N_GROUPS - 1
+        t0 = n * TOKEN_TILES
+        rope_products(t0)
+        multiply(t0 + 3)
+        rope_products(t0 + 1)
+        rope_add(t0, nc.gpsimd)
+        sum_squares(t0)
+        root_mean_square(n, [0])
+        rope_products(t0 + 2)
+        rope_add(t0 + 1, nc.gpsimd)
+        sum_squares(t0 + 1)
+        root_mean_square(n, [1])
+        rope_products(t0 + 3)
+        rope_add(t0 + 2, nc.vector)
+        sum_squares(t0 + 2)
+        root_mean_square(n, [2])
+        rope_add(t0 + 3, nc.vector)
+        sum_squares(t0 + 3)
+        root_mean_square(n, [3])
+        for tt in all_tiles:
+            invert(n, [tt])
+            normalise(t0 + tt, True)
+            store(t0 + tt)

@@ -29,11 +29,11 @@ N_TILES = N_GROUPS * TOKEN_TILES
 EPS = 2.0 ** -23
 
 X_ON_SCALAR = (0, 1, 2, 3)
-FUSED_TILES = (2, 3)
+FUSED = (1, 0, 0, 2)
 
 
 def fused_on_vector(ti):
-    return ti % 4 in FUSED_TILES or ti >= N_TILES - 4
+    return 2 if ti >= N_TILES - 4 else FUSED[ti % 4]
 
 
 def tile_attention_pa_kernel(
@@ -226,16 +226,14 @@ def tile_attention_pa_kernel(
             prod_of[ti] = prod
 
         def rope_add(ti, adder):
-            prod = prod_of[ti]
+            halves = prod_of[ti][:].rearrange("p w (h f j) -> p w h f j", f=2, j=HALF)
             roped_of[ti] = work.tile([P, GROUP], F32, name="roped", bufs=12)
-            parts = "p (h f j) -> p h f j"
-            same = prod[:, 0, :].rearrange(parts, f=2, j=HALF)
-            cross = prod[:, 1, :].rearrange(parts, f=2, j=HALF)
-            out = roped_of[ti][:].rearrange(parts, f=2, j=HALF)
-            for f in range(2):
-                adder.tensor_tensor(
-                    out=out[:, :, f, :], in0=same[:, :, f, :], in1=cross[:, :, 1 - f, :], op=ALU.add
-                )
+            adder.tensor_tensor(
+                out=roped_of[ti][:].rearrange("p (h w j) -> p w h j", w=2, j=HALF),
+                in0=halves[:, :, :, 0, :],
+                in1=halves[:, :, :, 1, :],
+                op=ALU.add,
+            )
 
         def sum_squares(ti):
             i, tt = ti // TOKEN_TILES, ti % TOKEN_TILES
@@ -264,11 +262,10 @@ def tile_attention_pa_kernel(
             nc.vector.reciprocal(out=inv_of[i][:, cols], in_=rms_of[i][:, cols])
 
         def weigh(ti):
+            m = 2 - fused_on_vector(ti)
+            part = roped_of[ti][:, 0 : m * PAIR * HEAD].rearrange("p (m h d) -> p m h d", m=m, d=HEAD)
             nc.gpsimd.tensor_tensor(
-                out=roped_of[ti][:].rearrange("p (m h d) -> p m h d", m=2, d=HEAD),
-                in0=roped_of[ti][:].rearrange("p (m h d) -> p m h d", m=2, d=HEAD),
-                in1=norm_rows[:].unsqueeze(2).to_broadcast([P, 2, PAIR, HEAD]),
-                op=ALU.mult,
+                out=part, in0=part, in1=norm_rows[:, 0:m, :].unsqueeze(2).to_broadcast([P, m, PAIR, HEAD]), op=ALU.mult
             )
 
         def store(ti):
@@ -283,7 +280,8 @@ def tile_attention_pa_kernel(
         def normalise(ti, fused):
             i, tt = ti // TOKEN_TILES, ti % TOKEN_TILES
             roped = roped_of[ti]
-            for h in range(2 * PAIR):
+            split = (2 - fused_on_vector(ti)) * PAIR
+            for h in range(split, 2 * PAIR) if fused else range(split):
                 cols = slice(h * HEAD, (h + 1) * HEAD)
                 inv = inv_of[i][:, tt * 4 + h : tt * 4 + h + 1]
                 if fused:
@@ -298,11 +296,11 @@ def tile_attention_pa_kernel(
             for th in range(2):
                 t = const.tile([P, 2, HEAD], BF16, name="rope_tab%d" % th)
                 nc.gpsimd.tensor_copy(out=t[:, 0, 0:HALF], in_=trig[:, 0, th, :])
-                nc.gpsimd.tensor_copy(out=t[:, 0, HALF:HEAD], in_=trig[:, 0, th, :])
-                nc.gpsimd.tensor_copy(out=t[:, 1, 0:HALF], in_=trig[:, 1, th, :])
                 nc.gpsimd.tensor_scalar(
-                    out=t[:, 1, HALF:HEAD], in0=trig[:, 1, th, :], scalar1=-1.0, scalar2=0.0, op0=ALU.mult, op1=ALU.add
+                    out=t[:, 0, HALF:HEAD], in0=trig[:, 1, th, :], scalar1=-1.0, scalar2=0.0, op0=ALU.mult, op1=ALU.add
                 )
+                nc.gpsimd.tensor_copy(out=t[:, 1, 0:HALF], in_=trig[:, 1, th, :])
+                nc.gpsimd.tensor_copy(out=t[:, 1, HALF:HEAD], in_=trig[:, 0, th, :])
                 rope_tab.append(t)
 
         def park_norm_weights():
@@ -372,12 +370,11 @@ def tile_attention_pa_kernel(
                 for tt in all_tiles:
                     if fused_on_vector(t0 - 4 + tt):
                         normalise(t0 - 4 + tt, True)
-                        store(t0 - 4 + tt)
                 for tt in all_tiles:
-                    if not fused_on_vector(t0 - 4 + tt):
+                    if fused_on_vector(t0 - 4 + tt) < 2:
                         normalise(t0 - 4 + tt, False)
                         weigh(t0 - 4 + tt)
-                        store(t0 - 4 + tt)
+                    store(t0 - 4 + tt)
             if last:
                 continue
             if halves:

@@ -30,10 +30,16 @@ EPS = 2.0 ** -23
 
 X_ON_SCALAR = (0, 1, 2, 3)
 FUSED = (1, 0, 0, 2)
+AHEAD = (1, 2, 3, 4)
+
+
+FUSED_MORE = (1, 0, 1, 2)
 
 
 def fused_on_vector(ti):
-    return 2 if ti >= N_TILES - 4 else FUSED[ti % 4]
+    if ti >= N_TILES - 4:
+        return 2
+    return FUSED_MORE[ti % 4] if ti // 4 + 2 in AHEAD else FUSED[ti % 4]
 
 
 def tile_attention_pa_kernel(
@@ -56,10 +62,19 @@ def tile_attention_pa_kernel(
         x_flat = x.flatten_outer_dims()
         x_rows = []
 
-        def load_group(i):
+        def load_ahead(i):
             rows = slice(i * PAIR * P, (i + 1) * PAIR * P)
             q_bytes[i] = raw.tile([P, PAIR, K], U8, name="q_bytes%d" % i)
-            nc.sync.dma_start(out=q_bytes[i][:], in_=Wq_bytes[rows, :].rearrange("(r p) k -> p r k", p=P))
+            nc.sync.dma_start(
+                out=q_bytes[i][:, :, 0:K_PASS], in_=Wq_bytes[rows, 0:K_PASS].rearrange("(r p) k -> p r k", p=P)
+            )
+
+        def load_group(i):
+            rows = slice(i * PAIR * P, (i + 1) * PAIR * P)
+            cols = slice(K_PASS if i in AHEAD else 0, K)
+            if i not in AHEAD:
+                q_bytes[i] = raw.tile([P, PAIR, K], U8, name="q_bytes%d" % i)
+            nc.sync.dma_start(out=q_bytes[i][:, :, cols], in_=Wq_bytes[rows, cols].rearrange("(r p) k -> p r k", p=P))
             k_rows[i] = raw.tile([P, PAIR, K], BF16, name="k_rows%d" % i)
             nc.sync.dma_start(out=k_rows[i][:], in_=Wk[rows, :].rearrange("(r p) k -> p r k", p=P))
 
@@ -86,6 +101,10 @@ def tile_attention_pa_kernel(
         nc.sync.dma_start(out=trig[:, 1, :, :], in_=sin.rearrange("(th p) j -> p th j", p=P))
         load_first(k_rows[0], Wk, 1)
         load_x(1)
+        scale_first = const.tile([P, K_PASS], F32, name="scale_first")
+        nc.sync.dma_start(out=scale_first[:], in_=Wq_scale[0, 0:K_PASS].partition_broadcast(P))
+        for i in AHEAD:
+            load_ahead(i)
         nc.sync.dma_start(out=norm_rows[:, 0, :], in_=q_norm_w.partition_broadcast(P))
         nc.sync.dma_start(out=norm_rows[:, 1, :], in_=k_norm_w.partition_broadcast(P))
         load_x(2)
@@ -153,7 +172,19 @@ def tile_attention_pa_kernel(
 
         def cast_half(hi):
             i, j = hi // 4, hi % 4
-            cast(nc.scalar.copy, PAIR * i + j % 2, j // 2, 2)
+            if i in AHEAD and j // 2 == 0:
+                cast(nc.scalar.copy, PAIR * i + j % 2, 1, PASSES)
+            else:
+                cast(nc.scalar.copy, PAIR * i + j % 2, j // 2, 2)
+
+        q_first = {}
+
+        def widen_first(i, r):
+            if i not in q_first:
+                q_first[i] = const.tile([P, PAIR, K_PASS], BF16, name="q_first%d" % i)
+            nc.vector.tensor_tensor(
+                out=q_first[i][:, r, :], in0=q_bytes[i][:, r, 0:K_PASS].bitcast(FP8), in1=scale_first[:], op=ALU.mult
+            )
 
         grouped_of = {}
         banks_of = {}
@@ -162,7 +193,10 @@ def tile_attention_pa_kernel(
         def turn_q(pi):
             i, g = pi // PASSES, pi % PASSES
             grouped_of[pi] = work.tile([P, K], BF16, name="grouped", tag="grouped", bufs=5, align_bytes=64)
-            banks_of[pi] = [turn([(q_wide[PAIR * i][:], g), (q_wide[PAIR * i + 1][:], g)])]
+            if g == 0 and i in AHEAD:
+                banks_of[pi] = [turn([(q_first[i][:, 0, :], 0), (q_first[i][:, 1, :], 0)])]
+            else:
+                banks_of[pi] = [turn([(q_wide[PAIR * i][:], g), (q_wide[PAIR * i + 1][:], g)])]
 
         def turn_k(pi):
             i, g = pi // PASSES, pi % PASSES
@@ -173,7 +207,10 @@ def tile_attention_pa_kernel(
             turn_k(pi)
 
         def empty_q(pi):
-            scale_out(banks_of[pi][0], grouped_of[pi], pi % PASSES)
+            if pi % PASSES == 0 and pi // PASSES in AHEAD:
+                copy_out(nc.scalar.copy, banks_of[pi][0], grouped_of[pi], 0)
+            else:
+                scale_out(banks_of[pi][0], grouped_of[pi], pi % PASSES)
 
         def empty_k(pi):
             copy_out(nc.scalar.copy, banks_of[pi][1], grouped_of[pi], 1)
@@ -227,7 +264,7 @@ def tile_attention_pa_kernel(
 
         def rope_add(ti, adder):
             halves = prod_of[ti][:].rearrange("p w (h f j) -> p w h f j", f=2, j=HALF)
-            roped_of[ti] = work.tile([P, GROUP], F32, name="roped", bufs=12)
+            roped_of[ti] = work.tile([P, GROUP], F32, name="roped", bufs=10)
             adder.tensor_tensor(
                 out=roped_of[ti][:].rearrange("p (h w j) -> p w h j", w=2, j=HALF),
                 in0=halves[:, :, :, 0, :],
@@ -337,6 +374,7 @@ def tile_attention_pa_kernel(
         turn_k(3)
         empty_k(2)
         empty_k(3)
+        widen_first(1, 0)
         quantise_x(0)
         turn_x(1)
         turn_x(2)
@@ -352,9 +390,16 @@ def tile_attention_pa_kernel(
                 turn_x(3)
             multiply(t0)
             if n == 0:
+                widen_first(1, 1)
+                widen_first(2, 0)
                 quantise_x(1)
+                widen_first(2, 1)
+                widen_first(3, 0)
                 quantise_x(2)
+                widen_first(3, 1)
+                widen_first(4, 0)
                 quantise_x(3)
+                widen_first(4, 1)
                 cast_half(4)
                 cast_half(5)
             multiply(t0 + 1)

@@ -150,7 +150,7 @@ def tile_attention_pa_kernel(
         x_grouped = {}
 
         def turn_x(tt):
-            grouped = work.tile([P, K], BF16, name="x_grouped", tag="grouped", bufs=5, align_bytes=64)
+            grouped = work.tile([P, K], BF16, name="x_grouped", tag="grouped", bufs=8, align_bytes=64)
             rows = x_rows[tt][:]
             copy_out(nc.scalar.copy, turn([(rows, 0), (rows, 1)]), grouped, 0)
             copy_out(nc.scalar.copy if tt in X_ON_SCALAR else nc.vector.tensor_copy, turn([(rows, 2), (rows, 3)]), grouped, 1)
@@ -192,7 +192,7 @@ def tile_attention_pa_kernel(
 
         def turn_q(pi):
             i, g = pi // PASSES, pi % PASSES
-            grouped_of[pi] = work.tile([P, K], BF16, name="grouped", tag="grouped", bufs=5, align_bytes=64)
+            grouped_of[pi] = work.tile([P, K], BF16, name="grouped", tag="grouped", bufs=8, align_bytes=64)
             if g == 0 and i in AHEAD:
                 banks_of[pi] = [turn([(q_first[i][:, 0, :], 0), (q_first[i][:, 1, :], 0)])]
             else:
@@ -218,8 +218,8 @@ def tile_attention_pa_kernel(
         def quantise_pass(pi):
             i, g = pi // PASSES, pi % PASSES
             if g == 0:
-                codes = work.tile([P, PASSES, GROUP], U32, name="w_codes", bufs=3, align_bytes=64)
-                scales = work.tile([P, PASSES, GROUP], U8, name="w_scales", bufs=3, align_bytes=64)
+                codes = work.tile([P, PASSES, GROUP], U32, name="w_codes", bufs=2, align_bytes=64)
+                scales = work.tile([P, PASSES, GROUP], U8, name="w_scales", bufs=2, align_bytes=64)
                 codes_of[i] = (codes, scales)
             codes, scales = codes_of[i]
             nc.vector.quantize_mx(

@@ -29,17 +29,7 @@ N_TILES = N_GROUPS * TOKEN_TILES
 EPS = 2.0 ** -23
 
 X_ON_SCALAR = (0, 1, 2, 3)
-FUSED = (1, 0, 0, 2)
-AHEAD = (1, 2, 3, 4)
-
-
-FUSED_MORE = (1, 0, 1, 2)
-
-
-def fused_on_vector(ti):
-    if ti >= N_TILES - 4:
-        return 2
-    return FUSED_MORE[ti % 4] if ti // 4 + 2 in AHEAD else FUSED[ti % 4]
+AHEAD = ()
 
 
 def tile_attention_pa_kernel(
@@ -93,6 +83,7 @@ def tile_attention_pa_kernel(
 
         trig = const.tile([P, 2, 2, HALF], BF16, name="trig")
         norm_rows = const.tile([P, 2, HEAD], BF16, name="norm_rows")
+        norm_wide = const.tile([P, 2, PAIR, HEAD], BF16, name="norm_wide")
         load_first(q_bytes[0], Wq_bytes, 0)
         load_first(q_bytes[0], Wq_bytes, 1)
         load_first(k_rows[0], Wk, 0)
@@ -180,6 +171,8 @@ def tile_attention_pa_kernel(
         q_first = {}
 
         def widen_first(i, r):
+            if i not in AHEAD:
+                return
             if i not in q_first:
                 q_first[i] = const.tile([P, PAIR, K_PASS], BF16, name="q_first%d" % i)
             nc.vector.tensor_tensor(
@@ -253,20 +246,20 @@ def tile_attention_pa_kernel(
 
         def rope_products(ti):
             shape = [P, 2, 2 * PAIR, HEAD]
-            prod = work.tile([P, 2, GROUP], F32, name="prod", bufs=4)
+            if ti % 2 == 0:
+                prod_of[ti // 2] = work.tile([P, 2, 2, GROUP], F32, name="prod", bufs=2)
             nc.vector.tensor_tensor(
-                out=prod[:].rearrange("p w (h d) -> p w h d", d=HEAD),
+                out=prod_of[ti // 2][:, :, ti % 2, :].rearrange("p w (h d) -> p w h d", d=HEAD),
                 in0=acc_of[ti][:].rearrange("p (h d) -> p h d", d=HEAD).unsqueeze(1).to_broadcast(shape),
                 in1=rope_tab[ti % 2][:].unsqueeze(2).to_broadcast(shape),
                 op=ALU.mult,
             )
-            prod_of[ti] = prod
 
-        def rope_add(ti, adder):
-            halves = prod_of[ti][:].rearrange("p w (h f j) -> p w h f j", f=2, j=HALF)
-            roped_of[ti] = work.tile([P, GROUP], F32, name="roped", bufs=10)
+        def rope_add(pr, adder):
+            halves = prod_of[pr][:].rearrange("p w t (h f j) -> p w (t h) f j", f=2, j=HALF)
+            roped_of[pr] = work.tile([P, 2, GROUP], F32, name="roped", bufs=5)
             adder.tensor_tensor(
-                out=roped_of[ti][:].rearrange("p (h w j) -> p w h j", w=2, j=HALF),
+                out=roped_of[pr][:].rearrange("p t (h w j) -> p w (t h) j", w=2, j=HALF),
                 in0=halves[:, :, :, 0, :],
                 in1=halves[:, :, :, 1, :],
                 op=ALU.add,
@@ -283,7 +276,7 @@ def tile_attention_pa_kernel(
                 col = tt * 4 + h
                 nc.scalar.activation(
                     out=squares[:],
-                    in_=roped_of[ti][:, h * HEAD : (h + 1) * HEAD],
+                    in_=roped_of[ti // 2][:, ti % 2, h * HEAD : (h + 1) * HEAD],
                     func=ACT.Square,
                     accum_out=sumsq_of[i][:, col : col + 1],
                 )
@@ -298,12 +291,38 @@ def tile_attention_pa_kernel(
             cols = slice(tts[0] * 4, (tts[-1] + 1) * 4)
             nc.vector.reciprocal(out=inv_of[i][:, cols], in_=rms_of[i][:, cols])
 
-        def weigh(ti):
-            m = 2 - fused_on_vector(ti)
-            part = roped_of[ti][:, 0 : m * PAIR * HEAD].rearrange("p (m h d) -> p m h d", m=m, d=HEAD)
-            nc.gpsimd.tensor_tensor(
-                out=part, in0=part, in1=norm_rows[:, 0:m, :].unsqueeze(2).to_broadcast([P, m, PAIR, HEAD]), op=ALU.mult
+        def weigh(pr, tts, cols=slice(0, GROUP)):
+            part = roped_of[pr][:, tts, cols]
+            rows = norm_wide[:].rearrange("p m h d -> p (m h d)")[:, cols]
+            shape = [P, tts.stop - tts.start, cols.stop - cols.start]
+            nc.gpsimd.tensor_tensor(out=part, in0=part, in1=rows.unsqueeze(1).to_broadcast(shape), op=ALU.mult)
+
+        def weigh_on_vector(pr, tts, m):
+            cols = slice(m * PAIR * HEAD, (m + 1) * PAIR * HEAD)
+            part = roped_of[pr][:, tts, cols]
+            shape = [P, tts.stop - tts.start, PAIR * HEAD]
+            nc.vector.tensor_tensor(
+                out=part, in0=part, in1=norm_bank[:, m, :, :].rearrange("p h d -> p (h d)").unsqueeze(1).to_broadcast(shape), op=ALU.mult
             )
+
+        def normalise(ti):
+            i, tt = ti // TOKEN_TILES, ti % TOKEN_TILES
+            roped = roped_of[ti // 2][:, ti % 2, :]
+            for h in range(2 * PAIR):
+                cols = slice(h * HEAD, (h + 1) * HEAD)
+                inv = inv_of[i][:, tt * 4 + h : tt * 4 + h + 1]
+                nc.scalar.activation(out=roped[:, cols], in_=roped[:, cols], func=ACT.Copy, scale=inv)
+
+        def finish_on_vector(ti):
+            i, tt = ti // TOKEN_TILES, ti % TOKEN_TILES
+            roped = roped_of[ti // 2][:, ti % 2, :]
+            for h in range(2 * PAIR):
+                cols = slice(h * HEAD, (h + 1) * HEAD)
+                inv = inv_of[i][:, tt * 4 + h : tt * 4 + h + 1]
+                nc.vector.scalar_tensor_tensor(
+                    out=roped[:, cols], in0=roped[:, cols], scalar=inv, in1=norm_bank[:, h // PAIR, h % PAIR, :],
+                    op0=ALU.mult, op1=ALU.mult,
+                )
 
         def store(ti):
             i, tt = ti // TOKEN_TILES, ti % TOKEN_TILES
@@ -311,23 +330,8 @@ def tile_attention_pa_kernel(
             for m, dst in enumerate((out_0, out_1)):
                 nc.sync.dma_start(
                     out=dst[b, i * PAIR : (i + 1) * PAIR, th * P : (th + 1) * P, :].rearrange("h t d -> t h d"),
-                    in_=roped_of[ti][:, m * PAIR * HEAD : (m + 1) * PAIR * HEAD].rearrange("p (h d) -> p h d", d=HEAD),
+                    in_=roped_of[ti // 2][:, ti % 2, m * PAIR * HEAD : (m + 1) * PAIR * HEAD].rearrange("p (h d) -> p h d", d=HEAD),
                 )
-
-        def normalise(ti, fused):
-            i, tt = ti // TOKEN_TILES, ti % TOKEN_TILES
-            roped = roped_of[ti]
-            split = (2 - fused_on_vector(ti)) * PAIR
-            for h in range(split, 2 * PAIR) if fused else range(split):
-                cols = slice(h * HEAD, (h + 1) * HEAD)
-                inv = inv_of[i][:, tt * 4 + h : tt * 4 + h + 1]
-                if fused:
-                    nc.vector.scalar_tensor_tensor(
-                        out=roped[:, cols], in0=roped[:, cols], scalar=inv, in1=norm_bank[:, h // PAIR, :],
-                        op0=ALU.mult, op1=ALU.mult,
-                    )
-                else:
-                    nc.scalar.activation(out=roped[:, cols], in_=roped[:, cols], func=ACT.Copy, scale=inv)
 
         def make_tables():
             for th in range(2):
@@ -340,14 +344,19 @@ def tile_attention_pa_kernel(
                 nc.gpsimd.tensor_copy(out=t[:, 1, HALF:HEAD], in_=trig[:, 0, th, :])
                 rope_tab.append(t)
 
+        def widen_norm_weights():
+            for h in range(PAIR):
+                nc.scalar.copy(out=norm_wide[:, :, h, :], in_=norm_rows[:])
+
         def park_norm_weights():
             for m in range(2):
-                nc.tensor.matmul(
-                    out=norm_bank[:, m, :], lhsT=ident_bf[:], rhs=norm_rows[:, m, :], start=True, stop=True
-                )
+                for h in range(PAIR):
+                    nc.tensor.matmul(
+                        out=norm_bank[:, m, h, :], lhsT=ident_bf[:], rhs=norm_rows[:, m, :], start=True, stop=True
+                    )
 
         rope_tab = []
-        norm_bank = psum.tile([P, 2, HEAD], F32, name="norm_bank", tag="norm_bank", bufs=1)
+        norm_bank = psum.tile([P, 2, PAIR, HEAD], F32, name="norm_bank", tag="norm_bank", bufs=1)
         all_tiles = list(range(TOKEN_TILES))
 
         for g in range(2):
@@ -406,47 +415,57 @@ def tile_attention_pa_kernel(
             multiply(t0 + 2)
             if n == 0:
                 park_norm_weights()
+                widen_norm_weights()
                 turn_pass(4)
                 cast_half(6)
                 cast_half(7)
                 turn_pass(5)
             if n > 0:
                 invert(n - 1, all_tiles)
-                for tt in all_tiles:
-                    if fused_on_vector(t0 - 4 + tt):
-                        normalise(t0 - 4 + tt, True)
-                for tt in all_tiles:
-                    if fused_on_vector(t0 - 4 + tt) < 2:
-                        normalise(t0 - 4 + tt, False)
-                        weigh(t0 - 4 + tt)
+                last_pair = 2 * (n - 1) + 1
+                for tt in (2, 3):
+                    normalise(t0 - 4 + tt)
+                    weigh(last_pair, slice(tt - 2, tt - 1))
                     store(t0 - 4 + tt)
             if last:
+                for tt in (0, 1):
+                    normalise(t0 - 4 + tt)
+                    store(t0 - 4 + tt)
                 continue
             if halves:
                 cast_half(halves[0])
-            rope_products(t0)
+            if n > 0:
+                empty_q(nxt)
+                empty_k(nxt)
             multiply(t0 + 3)
-            rope_products(t0 + 1)
-            rope_add(t0, nc.gpsimd)
-            empty_q(nxt)
-            empty_k(nxt)
+            for tt in all_tiles:
+                rope_products(t0 + tt)
+            rope_add(2 * n, nc.gpsimd)
+            if n == 0:
+                empty_q(nxt)
+                empty_k(nxt)
             turn_pass(nxt + 2)
-            rope_add(t0 + 1, nc.gpsimd)
-            rope_products(t0 + 2)
+            if n > 0:
+                for tt in (0, 1):
+                    normalise(t0 - 4 + tt)
+                    store(t0 - 4 + tt)
             if halves:
                 cast_half(halves[1])
             empty_q(nxt + 1)
             empty_k(nxt + 1)
             turn_pass(nxt + 3)
             sum_squares(t0)
-            rope_add(t0 + 2, nc.gpsimd)
-            rope_products(t0 + 3)
+            rope_add(2 * n + 1, nc.gpsimd)
             empty_q(nxt + 2)
             empty_k(nxt + 2)
             sum_squares(t0 + 1)
-            rope_add(t0 + 3, nc.gpsimd)
+            if n + 2 in AHEAD:
+                weigh_on_vector(2 * n, slice(0, 2), 0)
+            else:
+                weigh(2 * n, slice(0, 2), slice(0, PAIR * HEAD))
             empty_q(nxt + 3)
             empty_k(nxt + 3)
+            weigh_on_vector(2 * n, slice(0, 2), 1)
             sum_squares(t0 + 2)
             sum_squares(t0 + 3)
             root_mean_square(n, all_tiles)
@@ -462,21 +481,22 @@ def tile_attention_pa_kernel(
         rope_products(t0)
         multiply(t0 + 3)
         rope_products(t0 + 1)
-        rope_add(t0, nc.gpsimd)
-        sum_squares(t0)
-        root_mean_square(n, [0])
+        rope_add(2 * n, nc.gpsimd)
         rope_products(t0 + 2)
-        rope_add(t0 + 1, nc.gpsimd)
+        sum_squares(t0)
         sum_squares(t0 + 1)
-        root_mean_square(n, [1])
+        root_mean_square(n, [0, 1])
         rope_products(t0 + 3)
-        rope_add(t0 + 2, nc.vector)
+        rope_add(2 * n + 1, nc.vector)
         sum_squares(t0 + 2)
         root_mean_square(n, [2])
-        rope_add(t0 + 3, nc.vector)
         sum_squares(t0 + 3)
         root_mean_square(n, [3])
-        for tt in all_tiles:
+        invert(n, [0, 1])
+        for tt in (0, 1):
+            finish_on_vector(t0 + tt)
+            store(t0 + tt)
+        for tt in (2, 3):
             invert(n, [tt])
-            normalise(t0 + tt, True)
+            finish_on_vector(t0 + tt)
             store(t0 + tt)

@@ -28,9 +28,6 @@ N_PASSES = N_GROUPS * PASSES
 N_TILES = N_GROUPS * TOKEN_TILES
 EPS = 2.0 ** -23
 
-X_ON_SCALAR = (0, 1, 2, 3)
-AHEAD = ()
-
 
 def tile_attention_pa_kernel(
     tc, x, sin, cos, Wq_bytes, Wq_scale, Wk, q_norm_w, k_norm_w, out_0, out_1
@@ -52,19 +49,10 @@ def tile_attention_pa_kernel(
         x_flat = x.flatten_outer_dims()
         x_rows = []
 
-        def load_ahead(i):
-            rows = slice(i * PAIR * P, (i + 1) * PAIR * P)
-            q_bytes[i] = raw.tile([P, PAIR, K], U8, name="q_bytes%d" % i)
-            nc.sync.dma_start(
-                out=q_bytes[i][:, :, 0:K_PASS], in_=Wq_bytes[rows, 0:K_PASS].rearrange("(r p) k -> p r k", p=P)
-            )
-
         def load_group(i):
             rows = slice(i * PAIR * P, (i + 1) * PAIR * P)
-            cols = slice(K_PASS if i in AHEAD else 0, K)
-            if i not in AHEAD:
-                q_bytes[i] = raw.tile([P, PAIR, K], U8, name="q_bytes%d" % i)
-            nc.sync.dma_start(out=q_bytes[i][:, :, cols], in_=Wq_bytes[rows, cols].rearrange("(r p) k -> p r k", p=P))
+            q_bytes[i] = raw.tile([P, PAIR, K], U8, name="q_bytes%d" % i)
+            nc.sync.dma_start(out=q_bytes[i][:], in_=Wq_bytes[rows, :].rearrange("(r p) k -> p r k", p=P))
             k_rows[i] = raw.tile([P, PAIR, K], BF16, name="k_rows%d" % i)
             nc.sync.dma_start(out=k_rows[i][:], in_=Wk[rows, :].rearrange("(r p) k -> p r k", p=P))
 
@@ -74,32 +62,33 @@ def tile_attention_pa_kernel(
             x_rows.append(t)
 
         q_bytes[0] = raw.tile([P, PAIR, K], U8, name="q_bytes0")
-        k_rows[0] = raw.tile([P, PAIR, K], BF16, name="k_rows0")
+        k_half = []
+        for half in range(2):
+            k_half.append(raw.tile([P, PAIR, K // 2], BF16, name="k_half%d" % half))
         first = slice(0, PAIR * P)
 
         def load_first(tile, src, half):
             cols = slice(half * K // 2, (half + 1) * K // 2)
-            nc.sync.dma_start(out=tile[:, :, cols], in_=src[first, cols].rearrange("(r p) k -> p r k", p=P))
+            nc.sync.dma_start(out=tile, in_=src[first, cols].rearrange("(r p) k -> p r k", p=P))
 
-        trig = const.tile([P, 2, 2, HALF], BF16, name="trig")
+        rope_tab = const.tile([P, 2, 2, HEAD], BF16, name="rope_tab")
         norm_rows = const.tile([P, 2, HEAD], BF16, name="norm_rows")
         norm_wide = const.tile([P, 2, PAIR, HEAD], BF16, name="norm_wide")
-        load_first(q_bytes[0], Wq_bytes, 0)
-        load_first(q_bytes[0], Wq_bytes, 1)
-        load_first(k_rows[0], Wk, 0)
+        load_first(q_bytes[0][:, :, 0 : K // 2], Wq_bytes, 0)
+        load_first(q_bytes[0][:, :, K // 2 : K], Wq_bytes, 1)
+        load_first(k_half[0][:], Wk, 0)
         load_x(0)
-        nc.sync.dma_start(out=trig[:, 0, :, :], in_=cos.rearrange("(th p) j -> p th j", p=P))
-        nc.sync.dma_start(out=trig[:, 1, :, :], in_=sin.rearrange("(th p) j -> p th j", p=P))
-        load_first(k_rows[0], Wk, 1)
+        load_first(k_half[1][:], Wk, 1)
         load_x(1)
-        scale_first = const.tile([P, K_PASS], F32, name="scale_first")
-        nc.sync.dma_start(out=scale_first[:], in_=Wq_scale[0, 0:K_PASS].partition_broadcast(P))
-        for i in AHEAD:
-            load_ahead(i)
-        nc.sync.dma_start(out=norm_rows[:, 0, :], in_=q_norm_w.partition_broadcast(P))
-        nc.sync.dma_start(out=norm_rows[:, 1, :], in_=k_norm_w.partition_broadcast(P))
+        nc.sync.dma_start(out=rope_tab[:, :, 1, 0:HALF], in_=sin.rearrange("(th p) j -> p th j", p=P))
+        for w in range(2):
+            nc.sync.dma_start(
+                out=rope_tab[:, :, w, w * HALF : (w + 1) * HALF], in_=cos.rearrange("(th p) j -> p th j", p=P)
+            )
         load_x(2)
         load_x(3)
+        nc.sync.dma_start(out=norm_rows[:, 0, :], in_=q_norm_w.partition_broadcast(P))
+        nc.sync.dma_start(out=norm_rows[:, 1, :], in_=k_norm_w.partition_broadcast(P))
         for i in range(1, N_GROUPS):
             load_group(i)
 
@@ -113,8 +102,8 @@ def tile_attention_pa_kernel(
         warm = const.tile([P, 1], F32, name="warm")
         nc.scalar.activation(out=warm[:], in_=one[:], func=ACT.Sqrt)
 
-        def turn(sources):
-            bank = psum.tile([P, 2, 2, P], F32, name="turned", tag="turned", bufs=4)
+        def turn(sources, tag="turned", bufs=4):
+            bank = psum.tile([P, 2, 2, P], F32, name="turned", tag=tag, bufs=bufs)
             for s, (rows, g) in enumerate(sources):
                 words = rows.bitcast(F32)
                 for u in range(2):
@@ -143,8 +132,9 @@ def tile_attention_pa_kernel(
         def turn_x(tt):
             grouped = work.tile([P, K], BF16, name="x_grouped", tag="grouped", bufs=8, align_bytes=64)
             rows = x_rows[tt][:]
-            copy_out(nc.scalar.copy, turn([(rows, 0), (rows, 1)]), grouped, 0)
-            copy_out(nc.scalar.copy if tt in X_ON_SCALAR else nc.vector.tensor_copy, turn([(rows, 2), (rows, 3)]), grouped, 1)
+            banks = ("acc", 3) if tt < 2 else ("turned", 4)
+            copy_out(nc.scalar.copy, turn([(rows, 0), (rows, 1)], *banks), grouped, 0)
+            copy_out(nc.scalar.copy, turn([(rows, 2), (rows, 3)], *banks), grouped, 1)
             x_grouped[tt] = grouped
 
         def quantise_x(tt):
@@ -163,21 +153,7 @@ def tile_attention_pa_kernel(
 
         def cast_half(hi):
             i, j = hi // 4, hi % 4
-            if i in AHEAD and j // 2 == 0:
-                cast(nc.scalar.copy, PAIR * i + j % 2, 1, PASSES)
-            else:
-                cast(nc.scalar.copy, PAIR * i + j % 2, j // 2, 2)
-
-        q_first = {}
-
-        def widen_first(i, r):
-            if i not in AHEAD:
-                return
-            if i not in q_first:
-                q_first[i] = const.tile([P, PAIR, K_PASS], BF16, name="q_first%d" % i)
-            nc.vector.tensor_tensor(
-                out=q_first[i][:, r, :], in0=q_bytes[i][:, r, 0:K_PASS].bitcast(FP8), in1=scale_first[:], op=ALU.mult
-            )
+            cast(nc.scalar.copy, PAIR * i + j % 2, j // 2, 2)
 
         grouped_of = {}
         banks_of = {}
@@ -186,24 +162,19 @@ def tile_attention_pa_kernel(
         def turn_q(pi):
             i, g = pi // PASSES, pi % PASSES
             grouped_of[pi] = work.tile([P, K], BF16, name="grouped", tag="grouped", bufs=8, align_bytes=64)
-            if g == 0 and i in AHEAD:
-                banks_of[pi] = [turn([(q_first[i][:, 0, :], 0), (q_first[i][:, 1, :], 0)])]
-            else:
-                banks_of[pi] = [turn([(q_wide[PAIR * i][:], g), (q_wide[PAIR * i + 1][:], g)])]
+            banks_of[pi] = [turn([(q_wide[PAIR * i][:], g), (q_wide[PAIR * i + 1][:], g)])]
 
         def turn_k(pi):
             i, g = pi // PASSES, pi % PASSES
-            banks_of[pi].append(turn([(k_rows[i][:, 0, :], g), (k_rows[i][:, 1, :], g)]))
+            rows, gg = (k_rows[i], g) if i > 0 else (k_half[g // 2], g % 2)
+            banks_of[pi].append(turn([(rows[:, 0, :], gg), (rows[:, 1, :], gg)]))
 
         def turn_pass(pi):
             turn_q(pi)
             turn_k(pi)
 
         def empty_q(pi):
-            if pi % PASSES == 0 and pi // PASSES in AHEAD:
-                copy_out(nc.scalar.copy, banks_of[pi][0], grouped_of[pi], 0)
-            else:
-                scale_out(banks_of[pi][0], grouped_of[pi], pi % PASSES)
+            scale_out(banks_of[pi][0], grouped_of[pi], pi % PASSES)
 
         def empty_k(pi):
             copy_out(nc.scalar.copy, banks_of[pi][1], grouped_of[pi], 1)
@@ -246,20 +217,22 @@ def tile_attention_pa_kernel(
 
         def rope_products(ti):
             shape = [P, 2, 2 * PAIR, HEAD]
-            if ti % 2 == 0:
-                prod_of[ti // 2] = work.tile([P, 2, 2, GROUP], F32, name="prod", bufs=2)
+            if ti % 2 == 0 or ti > N_TILES - 4:
+                prod_of[ti // 2] = work.tile([P, 2, 2, GROUP], F32, name="prod", bufs=3)
             nc.vector.tensor_tensor(
                 out=prod_of[ti // 2][:, :, ti % 2, :].rearrange("p w (h d) -> p w h d", d=HEAD),
                 in0=acc_of[ti][:].rearrange("p (h d) -> p h d", d=HEAD).unsqueeze(1).to_broadcast(shape),
-                in1=rope_tab[ti % 2][:].unsqueeze(2).to_broadcast(shape),
+                in1=rope_tab[:, ti % 2, :, :].unsqueeze(2).to_broadcast(shape),
                 op=ALU.mult,
             )
 
-        def rope_add(pr, adder):
-            halves = prod_of[pr][:].rearrange("p w t (h f j) -> p w (t h) f j", f=2, j=HALF)
-            roped_of[pr] = work.tile([P, 2, GROUP], F32, name="roped", bufs=5)
+        def rope_add(tiles, adder):
+            pr, ts = tiles[0] // 2, slice(tiles[0] % 2, tiles[-1] % 2 + 1)
+            if ts.start == 0:
+                roped_of[pr] = work.tile([P, 2, GROUP], F32, name="roped", bufs=5)
+            halves = prod_of[pr][:, :, ts, :].rearrange("p w t (h f j) -> p w (t h) f j", f=2, j=HALF)
             adder.tensor_tensor(
-                out=roped_of[pr][:].rearrange("p t (h w j) -> p w (t h) j", w=2, j=HALF),
+                out=roped_of[pr][:, ts, :].rearrange("p t (h w j) -> p w (t h) j", w=2, j=HALF),
                 in0=halves[:, :, :, 0, :],
                 in1=halves[:, :, :, 1, :],
                 op=ALU.add,
@@ -297,12 +270,10 @@ def tile_attention_pa_kernel(
             shape = [P, tts.stop - tts.start, cols.stop - cols.start]
             nc.gpsimd.tensor_tensor(out=part, in0=part, in1=rows.unsqueeze(1).to_broadcast(shape), op=ALU.mult)
 
-        def weigh_on_vector(pr, tts, m):
-            cols = slice(m * PAIR * HEAD, (m + 1) * PAIR * HEAD)
-            part = roped_of[pr][:, tts, cols]
-            shape = [P, tts.stop - tts.start, PAIR * HEAD]
+        def weigh_on_vector(pr, t):
+            part = roped_of[pr][:, t, :]
             nc.vector.tensor_tensor(
-                out=part, in0=part, in1=norm_bank[:, m, :, :].rearrange("p h d -> p (h d)").unsqueeze(1).to_broadcast(shape), op=ALU.mult
+                out=part, in0=part, in1=norm_bank[:].rearrange("p m h d -> p (m h d)"), op=ALU.mult
             )
 
         def normalise(ti):
@@ -333,17 +304,6 @@ def tile_attention_pa_kernel(
                     in_=roped_of[ti // 2][:, ti % 2, m * PAIR * HEAD : (m + 1) * PAIR * HEAD].rearrange("p (h d) -> p h d", d=HEAD),
                 )
 
-        def make_tables():
-            for th in range(2):
-                t = const.tile([P, 2, HEAD], BF16, name="rope_tab%d" % th)
-                nc.gpsimd.tensor_copy(out=t[:, 0, 0:HALF], in_=trig[:, 0, th, :])
-                nc.gpsimd.tensor_scalar(
-                    out=t[:, 0, HALF:HEAD], in0=trig[:, 1, th, :], scalar1=-1.0, scalar2=0.0, op0=ALU.mult, op1=ALU.add
-                )
-                nc.gpsimd.tensor_copy(out=t[:, 1, 0:HALF], in_=trig[:, 1, th, :])
-                nc.gpsimd.tensor_copy(out=t[:, 1, HALF:HEAD], in_=trig[:, 0, th, :])
-                rope_tab.append(t)
-
         def widen_norm_weights():
             for h in range(PAIR):
                 nc.scalar.copy(out=norm_wide[:, :, h, :], in_=norm_rows[:])
@@ -355,38 +315,36 @@ def tile_attention_pa_kernel(
                         out=norm_bank[:, m, h, :], lhsT=ident_bf[:], rhs=norm_rows[:, m, :], start=True, stop=True
                     )
 
-        rope_tab = []
         norm_bank = psum.tile([P, 2, PAIR, HEAD], F32, name="norm_bank", tag="norm_bank", bufs=1)
         all_tiles = list(range(TOKEN_TILES))
 
-        for g in range(2):
-            for r in range(PAIR):
-                cast(nc.vector.tensor_copy, r, g, PASSES)
-        for g in range(2, PASSES):
+        for r in range(PAIR):
+            cast(nc.vector.tensor_copy, r, 0, PASSES)
+        for g in range(1, PASSES):
             for r in range(PAIR):
                 cast(nc.scalar.copy, r, g, PASSES)
-        make_tables()
+        nc.gpsimd.tensor_scalar(
+            out=rope_tab[:, :, 0, HALF:HEAD], in0=rope_tab[:, :, 1, 0:HALF], scalar1=-1.0, scalar2=0.0, op0=ALU.mult, op1=ALU.add
+        )
         turn_q(0)
         turn_q(1)
-        empty_q(0)
+        turn_q(2)
+        turn_q(3)
+        for g in range(PASSES):
+            empty_q(g)
         turn_k(0)
-        empty_q(1)
         turn_k(1)
         empty_k(0)
-        turn_q(2)
         empty_k(1)
-        turn_q(3)
-        empty_q(2)
-        empty_q(3)
         turn_x(0)
         turn_k(2)
         turn_k(3)
         empty_k(2)
         empty_k(3)
-        widen_first(1, 0)
         quantise_x(0)
         turn_x(1)
         turn_x(2)
+        turn_x(3)
 
         for n in range(N_GROUPS):
             t0 = n * TOKEN_TILES
@@ -395,31 +353,26 @@ def tile_attention_pa_kernel(
             last = n == N_GROUPS - 1
             for g in range(PASSES):
                 quantise_pass(n * PASSES + g)
-            if n == 0:
-                turn_x(3)
             multiply(t0)
             if n == 0:
-                widen_first(1, 1)
-                widen_first(2, 0)
-                quantise_x(1)
-                widen_first(2, 1)
-                widen_first(3, 0)
-                quantise_x(2)
-                widen_first(3, 1)
-                widen_first(4, 0)
-                quantise_x(3)
-                widen_first(4, 1)
-                cast_half(4)
-                cast_half(5)
-            multiply(t0 + 1)
-            multiply(t0 + 2)
-            if n == 0:
-                park_norm_weights()
-                widen_norm_weights()
+                for h in range(4, 8):
+                    cast_half(h)
+                for tt in (1, 2, 3):
+                    quantise_x(tt)
+                multiply(t0 + 1)
+                multiply(t0 + 2)
+                rope_products(t0)
+                multiply(t0 + 3)
+                rope_products(t0 + 1)
+                rope_products(t0 + 2)
                 turn_pass(4)
-                cast_half(6)
-                cast_half(7)
                 turn_pass(5)
+                park_norm_weights()
+            else:
+                multiply(t0 + 1)
+                multiply(t0 + 2)
+            if last:
+                continue
             if n > 0:
                 invert(n - 1, all_tiles)
                 last_pair = 2 * (n - 1) + 1
@@ -427,21 +380,17 @@ def tile_attention_pa_kernel(
                     normalise(t0 - 4 + tt)
                     weigh(last_pair, slice(tt - 2, tt - 1))
                     store(t0 - 4 + tt)
-            if last:
-                for tt in (0, 1):
-                    normalise(t0 - 4 + tt)
-                    store(t0 - 4 + tt)
-                continue
             if halves:
                 cast_half(halves[0])
             if n > 0:
                 empty_q(nxt)
                 empty_k(nxt)
-            multiply(t0 + 3)
-            for tt in all_tiles:
+                multiply(t0 + 3)
+            for tt in all_tiles if n > 0 else (3,):
                 rope_products(t0 + tt)
-            rope_add(2 * n, nc.gpsimd)
+            rope_add((t0, t0 + 1), nc.gpsimd)
             if n == 0:
+                widen_norm_weights()
                 empty_q(nxt)
                 empty_k(nxt)
             turn_pass(nxt + 2)
@@ -455,17 +404,14 @@ def tile_attention_pa_kernel(
             empty_k(nxt + 1)
             turn_pass(nxt + 3)
             sum_squares(t0)
-            rope_add(2 * n + 1, nc.gpsimd)
+            rope_add((t0 + 2, t0 + 3), nc.gpsimd)
             empty_q(nxt + 2)
             empty_k(nxt + 2)
             sum_squares(t0 + 1)
-            if n + 2 in AHEAD:
-                weigh_on_vector(2 * n, slice(0, 2), 0)
-            else:
-                weigh(2 * n, slice(0, 2), slice(0, PAIR * HEAD))
+            weigh(2 * n, slice(1, 2))
             empty_q(nxt + 3)
             empty_k(nxt + 3)
-            weigh_on_vector(2 * n, slice(0, 2), 1)
+            weigh_on_vector(2 * n, 0)
             sum_squares(t0 + 2)
             sum_squares(t0 + 3)
             root_mean_square(n, all_tiles)
@@ -478,25 +424,34 @@ def tile_attention_pa_kernel(
 
         n = N_GROUPS - 1
         t0 = n * TOKEN_TILES
-        rope_products(t0)
         multiply(t0 + 3)
-        rope_products(t0 + 1)
-        rope_add(2 * n, nc.gpsimd)
-        rope_products(t0 + 2)
-        sum_squares(t0)
-        sum_squares(t0 + 1)
-        root_mean_square(n, [0, 1])
-        rope_products(t0 + 3)
-        rope_add(2 * n + 1, nc.vector)
-        sum_squares(t0 + 2)
-        root_mean_square(n, [2])
-        sum_squares(t0 + 3)
-        root_mean_square(n, [3])
-        invert(n, [0, 1])
-        for tt in (0, 1):
-            finish_on_vector(t0 + tt)
+        invert(n - 1, all_tiles)
+        normalise(t0 - 2)
+        weigh(2 * n - 1, slice(0, 1))
+        finish_on_vector(t0 - 1)
+        for tt in (-1, -2):
             store(t0 + tt)
+        for tt in (0, 1):
+            normalise(t0 - 4 + tt)
+            store(t0 - 4 + tt)
+        for tt in (0, 1):
+            rope_products(t0 + tt)
+            rope_add((t0 + tt,), nc.gpsimd)
+            sum_squares(t0 + tt)
+            root_mean_square(n, [tt])
+        rope_products(t0 + 2)
+        invert(n, [0])
         for tt in (2, 3):
+            if tt == 3:
+                rope_products(t0 + 3)
+            rope_add((t0 + tt,), nc.vector)
+            sum_squares(t0 + tt)
+            root_mean_square(n, [tt])
+            if tt == 2:
+                normalise(t0)
+                weigh(2 * n, slice(0, 1))
+                store(t0)
+        for tt in (1, 2, 3):
             invert(n, [tt])
             finish_on_vector(t0 + tt)
             store(t0 + tt)

@@ -217,10 +217,12 @@ def tile_attention_pa_kernel(
 
         def rope_products(ti):
             shape = [P, 2, 2 * PAIR, HEAD]
-            if ti % 2 == 0 or ti > N_TILES - 4:
-                prod_of[ti // 2] = work.tile([P, 2, 2, GROUP], F32, name="prod", bufs=3)
+            if ti % 2 == 0 or ti > N_TILES - TOKEN_TILES:
+                prod_of[ti] = work.tile([P, 2, 2, GROUP], F32, name="prod", bufs=3)
+            else:
+                prod_of[ti] = prod_of[ti - 1]
             nc.vector.tensor_tensor(
-                out=prod_of[ti // 2][:, :, ti % 2, :].rearrange("p w (h d) -> p w h d", d=HEAD),
+                out=prod_of[ti][:, :, ti % 2, :].rearrange("p w (h d) -> p w h d", d=HEAD),
                 in0=acc_of[ti][:].rearrange("p (h d) -> p h d", d=HEAD).unsqueeze(1).to_broadcast(shape),
                 in1=rope_tab[:, ti % 2, :, :].unsqueeze(2).to_broadcast(shape),
                 op=ALU.mult,
@@ -230,7 +232,7 @@ def tile_attention_pa_kernel(
             pr, ts = tiles[0] // 2, slice(tiles[0] % 2, tiles[-1] % 2 + 1)
             if ts.start == 0:
                 roped_of[pr] = work.tile([P, 2, GROUP], F32, name="roped", bufs=5)
-            halves = prod_of[pr][:, :, ts, :].rearrange("p w t (h f j) -> p w (t h) f j", f=2, j=HALF)
+            halves = prod_of[tiles[0]][:, :, ts, :].rearrange("p w t (h f j) -> p w (t h) f j", f=2, j=HALF)
             adder.tensor_tensor(
                 out=roped_of[pr][:, ts, :].rearrange("p t (h w j) -> p w (t h) j", w=2, j=HALF),
                 in0=halves[:, :, :, 0, :],
@@ -245,7 +247,7 @@ def tile_attention_pa_kernel(
                 rms_of[i] = work.tile([P, 4 * TOKEN_TILES], F32, name="rms", bufs=3)
                 inv_of[i] = work.tile([P, 4 * TOKEN_TILES], F32, name="inv", bufs=3)
             for h in range(2 * PAIR):
-                squares = work.tile([P, HEAD], BF16, name="squares", bufs=2)
+                squares = work.tile([P, HEAD], BF16, name="squares", bufs=8)
                 col = tt * 4 + h
                 nc.scalar.activation(
                     out=squares[:],
@@ -440,18 +442,18 @@ def tile_attention_pa_kernel(
             sum_squares(t0 + tt)
             root_mean_square(n, [tt])
         rope_products(t0 + 2)
+        rope_products(t0 + 3)
         invert(n, [0])
         for tt in (2, 3):
-            if tt == 3:
-                rope_products(t0 + 3)
             rope_add((t0 + tt,), nc.vector)
             sum_squares(t0 + tt)
             root_mean_square(n, [tt])
             if tt == 2:
                 normalise(t0)
                 weigh(2 * n, slice(0, 1))
-                store(t0)
         for tt in (1, 2, 3):
             invert(n, [tt])
             finish_on_vector(t0 + tt)
             store(t0 + tt)
+            if tt == 2:
+                store(t0)

@@ -27,6 +27,7 @@ N_GROUPS = 8
 N_PASSES = N_GROUPS * PASSES
 N_TILES = N_GROUPS * TOKEN_TILES
 EPS = 2.0 ** -23
+FINISH_ORDER = (2, 0, 1, 3)
 
 
 def tile_attention_pa_kernel(
@@ -240,6 +241,12 @@ def tile_attention_pa_kernel(
                 op=ALU.add,
             )
 
+        def column(tt):
+            return 4 * FINISH_ORDER.index(tt)
+
+        def columns(tts):
+            return slice(column(tts[0]), column(tts[-1]) + 4)
+
         def sum_squares(ti):
             i, tt = ti // TOKEN_TILES, ti % TOKEN_TILES
             if tt == 0:
@@ -247,8 +254,8 @@ def tile_attention_pa_kernel(
                 rms_of[i] = work.tile([P, 4 * TOKEN_TILES], F32, name="rms", bufs=3)
                 inv_of[i] = work.tile([P, 4 * TOKEN_TILES], F32, name="inv", bufs=3)
             for h in range(2 * PAIR):
-                squares = work.tile([P, HEAD], BF16, name="squares", bufs=8)
-                col = tt * 4 + h
+                squares = work.tile([P, HEAD], BF16, name="squares", bufs=16)
+                col = column(tt) + h
                 nc.scalar.activation(
                     out=squares[:],
                     in_=roped_of[ti // 2][:, ti % 2, h * HEAD : (h + 1) * HEAD],
@@ -257,13 +264,13 @@ def tile_attention_pa_kernel(
                 )
 
         def root_mean_square(i, tts):
-            cols = slice(tts[0] * 4, (tts[-1] + 1) * 4)
+            cols = columns(tts)
             nc.scalar.activation(
                 out=rms_of[i][:, cols], in_=sumsq_of[i][:, cols], func=ACT.Sqrt, bias=EPS, scale=1.0 / HEAD
             )
 
         def invert(i, tts):
-            cols = slice(tts[0] * 4, (tts[-1] + 1) * 4)
+            cols = columns(tts)
             nc.vector.reciprocal(out=inv_of[i][:, cols], in_=rms_of[i][:, cols])
 
         def weigh(pr, tts, cols=slice(0, GROUP)):
@@ -283,7 +290,7 @@ def tile_attention_pa_kernel(
             roped = roped_of[ti // 2][:, ti % 2, :]
             for h in range(2 * PAIR):
                 cols = slice(h * HEAD, (h + 1) * HEAD)
-                inv = inv_of[i][:, tt * 4 + h : tt * 4 + h + 1]
+                inv = inv_of[i][:, column(tt) + h : column(tt) + h + 1]
                 nc.scalar.activation(out=roped[:, cols], in_=roped[:, cols], func=ACT.Copy, scale=inv)
 
         def finish_on_vector(ti):
@@ -291,7 +298,7 @@ def tile_attention_pa_kernel(
             roped = roped_of[ti // 2][:, ti % 2, :]
             for h in range(2 * PAIR):
                 cols = slice(h * HEAD, (h + 1) * HEAD)
-                inv = inv_of[i][:, tt * 4 + h : tt * 4 + h + 1]
+                inv = inv_of[i][:, column(tt) + h : column(tt) + h + 1]
                 nc.vector.scalar_tensor_tensor(
                     out=roped[:, cols], in0=roped[:, cols], scalar=inv, in1=norm_bank[:, h // PAIR, h % PAIR, :],
                     op0=ALU.mult, op1=ALU.mult,
@@ -318,7 +325,6 @@ def tile_attention_pa_kernel(
                     )
 
         norm_bank = psum.tile([P, 2, PAIR, HEAD], F32, name="norm_bank", tag="norm_bank", bufs=1)
-        all_tiles = list(range(TOKEN_TILES))
 
         for r in range(PAIR):
             cast(nc.vector.tensor_copy, r, 0, PASSES)
@@ -355,6 +361,10 @@ def tile_attention_pa_kernel(
             last = n == N_GROUPS - 1
             for g in range(PASSES):
                 quantise_pass(n * PASSES + g)
+                if n > 0 and g == 1:
+                    invert(n - 1, [2])
+            if n > 0:
+                invert(n - 1, [0, 1, 3])
             multiply(t0)
             if n == 0:
                 for h in range(4, 8):
@@ -376,28 +386,29 @@ def tile_attention_pa_kernel(
             if last:
                 continue
             if n > 0:
-                invert(n - 1, all_tiles)
-                last_pair = 2 * (n - 1) + 1
                 for tt in (2, 3):
                     normalise(t0 - 4 + tt)
-                    weigh(last_pair, slice(tt - 2, tt - 1))
+                    weigh(2 * n - 1, slice(tt - 2, tt - 1))
                     store(t0 - 4 + tt)
+                weigh_on_vector(2 * n - 2, 0)
+                cast_half(4 * (n + 1) + 3)
             if halves:
                 cast_half(halves[0])
             if n > 0:
-                empty_q(nxt)
-                empty_k(nxt)
+                rope_products(t0)
                 multiply(t0 + 3)
-            for tt in all_tiles if n > 0 else (3,):
-                rope_products(t0 + tt)
-            rope_add((t0, t0 + 1), nc.gpsimd)
-            if n == 0:
+                for tt in (1, 2, 3):
+                    rope_products(t0 + tt)
+            else:
+                rope_products(t0 + 3)
                 widen_norm_weights()
-                empty_q(nxt)
-                empty_k(nxt)
+            rope_add((t0, t0 + 1), nc.gpsimd)
+            rope_add((t0 + 2, t0 + 3), nc.gpsimd)
+            empty_q(nxt)
+            empty_k(nxt)
             turn_pass(nxt + 2)
             if n > 0:
-                for tt in (0, 1):
+                for tt in (1, 0):
                     normalise(t0 - 4 + tt)
                     store(t0 - 4 + tt)
             if halves:
@@ -406,20 +417,18 @@ def tile_attention_pa_kernel(
             empty_k(nxt + 1)
             turn_pass(nxt + 3)
             sum_squares(t0)
-            rope_add((t0 + 2, t0 + 3), nc.gpsimd)
-            empty_q(nxt + 2)
-            empty_k(nxt + 2)
             sum_squares(t0 + 1)
             weigh(2 * n, slice(1, 2))
+            empty_q(nxt + 2)
+            empty_k(nxt + 2)
             empty_q(nxt + 3)
-            empty_k(nxt + 3)
-            weigh_on_vector(2 * n, 0)
             sum_squares(t0 + 2)
+            empty_k(nxt + 3)
+            root_mean_square(n, [2])
             sum_squares(t0 + 3)
-            root_mean_square(n, all_tiles)
             if halves:
                 cast_half(halves[2])
-                cast_half(halves[3])
+            root_mean_square(n, [0, 1, 3])
             if n + 2 < N_GROUPS:
                 turn_pass(nxt + 4)
                 turn_pass(nxt + 5)
@@ -427,13 +436,13 @@ def tile_attention_pa_kernel(
         n = N_GROUPS - 1
         t0 = n * TOKEN_TILES
         multiply(t0 + 3)
-        invert(n - 1, all_tiles)
         normalise(t0 - 2)
         weigh(2 * n - 1, slice(0, 1))
         finish_on_vector(t0 - 1)
         for tt in (-1, -2):
             store(t0 + tt)
-        for tt in (0, 1):
+        weigh_on_vector(2 * n - 2, 0)
+        for tt in (1, 0):
             normalise(t0 - 4 + tt)
             store(t0 - 4 + tt)
         for tt in (0, 1):
@@ -443,16 +452,16 @@ def tile_attention_pa_kernel(
             root_mean_square(n, [tt])
         rope_products(t0 + 2)
         rope_products(t0 + 3)
-        invert(n, [0])
         for tt in (2, 3):
             rope_add((t0 + tt,), nc.vector)
             sum_squares(t0 + tt)
             root_mean_square(n, [tt])
-            if tt == 2:
-                normalise(t0)
-                weigh(2 * n, slice(0, 1))
+        invert(n, [0, 1])
+        weigh_on_vector(2 * n, 0)
+        normalise(t0)
         for tt in (1, 2, 3):
-            invert(n, [tt])
+            if tt > 1:
+                invert(n, [tt])
             finish_on_vector(t0 + tt)
             store(t0 + tt)
             if tt == 2:

@@ -98,10 +98,13 @@ def tile_attention_pa_kernel(
         ident_bf = const.tile([P, P], BF16, name="ident_bf")
         make_identity(nc, ident_bf[:])
 
+        zeros = const.tile([P, GROUP], BF16, name="zeros")
+        nc.vector.memset(zeros[:], 0.0)
+
         one = const.tile([P, 1], F32, name="one")
         nc.vector.memset(one[:], 1.0)
         warm = const.tile([P, 1], F32, name="warm")
-        nc.scalar.activation(out=warm[:], in_=one[:], func=ACT.Sqrt)
+        nc.scalar.activation(out=warm[:], in_=one[:], func=ACT.Abs_reciprocal_sqrt)
 
         def turn(sources, tag="turned", bufs=4):
             bank = psum.tile([P, 2, 2, P], F32, name="turned", tag=tag, bufs=bufs)
@@ -193,6 +196,11 @@ def tile_attention_pa_kernel(
 
         acc_of = {}
 
+        def keep_warm(times):
+            bank = psum.tile([P, GROUP], F32, name="warm_bank", tag="acc", bufs=3)
+            for r in range(times):
+                nc.tensor.matmul(out=bank[:], lhsT=ident_bf[:], rhs=zeros[:], start=True, stop=True)
+
         def multiply(ti):
             i, tt = ti // TOKEN_TILES, ti % TOKEN_TILES
             codes, scales = codes_of[i]
@@ -213,7 +221,6 @@ def tile_attention_pa_kernel(
         prod_of = {}
         roped_of = {}
         sumsq_of = {}
-        rms_of = {}
         inv_of = {}
 
         def rope_products(ti):
@@ -251,7 +258,6 @@ def tile_attention_pa_kernel(
             i, tt = ti // TOKEN_TILES, ti % TOKEN_TILES
             if tt == 0:
                 sumsq_of[i] = work.tile([P, 4 * TOKEN_TILES], F32, name="sumsq", bufs=3)
-                rms_of[i] = work.tile([P, 4 * TOKEN_TILES], F32, name="rms", bufs=3)
                 inv_of[i] = work.tile([P, 4 * TOKEN_TILES], F32, name="inv", bufs=3)
             for h in range(2 * PAIR):
                 squares = work.tile([P, HEAD], BF16, name="squares", bufs=16)
@@ -263,15 +269,11 @@ def tile_attention_pa_kernel(
                     accum_out=sumsq_of[i][:, col : col + 1],
                 )
 
-        def root_mean_square(i, tts):
+        def invert_root(i, tts):
             cols = columns(tts)
             nc.scalar.activation(
-                out=rms_of[i][:, cols], in_=sumsq_of[i][:, cols], func=ACT.Sqrt, bias=EPS, scale=1.0 / HEAD
+                out=inv_of[i][:, cols], in_=sumsq_of[i][:, cols], func=ACT.Abs_reciprocal_sqrt, bias=EPS, scale=1.0 / HEAD
             )
-
-        def invert(i, tts):
-            cols = columns(tts)
-            nc.vector.reciprocal(out=inv_of[i][:, cols], in_=rms_of[i][:, cols])
 
         def weigh(pr, tts, cols=slice(0, GROUP)):
             part = roped_of[pr][:, tts, cols]
@@ -326,11 +328,9 @@ def tile_attention_pa_kernel(
 
         norm_bank = psum.tile([P, 2, PAIR, HEAD], F32, name="norm_bank", tag="norm_bank", bufs=1)
 
-        for r in range(PAIR):
-            cast(nc.vector.tensor_copy, r, 0, PASSES)
-        for g in range(1, PASSES):
+        for g in range(PASSES):
             for r in range(PAIR):
-                cast(nc.scalar.copy, r, g, PASSES)
+                cast(nc.vector.tensor_copy if g < 2 else nc.scalar.copy, r, g, PASSES)
         nc.gpsimd.tensor_scalar(
             out=rope_tab[:, :, 0, HALF:HEAD], in0=rope_tab[:, :, 1, 0:HALF], scalar1=-1.0, scalar2=0.0, op0=ALU.mult, op1=ALU.add
         )
@@ -361,10 +361,6 @@ def tile_attention_pa_kernel(
             last = n == N_GROUPS - 1
             for g in range(PASSES):
                 quantise_pass(n * PASSES + g)
-                if n > 0 and g == 1:
-                    invert(n - 1, [2])
-            if n > 0:
-                invert(n - 1, [0, 1, 3])
             multiply(t0)
             if n == 0:
                 for h in range(4, 8):
@@ -397,6 +393,8 @@ def tile_attention_pa_kernel(
             if n > 0:
                 rope_products(t0)
                 multiply(t0 + 3)
+                turn_pass(nxt + 1)
+                keep_warm(2)
                 for tt in (1, 2, 3):
                     rope_products(t0 + tt)
             else:
@@ -424,14 +422,13 @@ def tile_attention_pa_kernel(
             empty_q(nxt + 3)
             sum_squares(t0 + 2)
             empty_k(nxt + 3)
-            root_mean_square(n, [2])
+            invert_root(n, [2])
             sum_squares(t0 + 3)
             if halves:
                 cast_half(halves[2])
-            root_mean_square(n, [0, 1, 3])
+            invert_root(n, [0, 1, 3])
             if n + 2 < N_GROUPS:
                 turn_pass(nxt + 4)
-                turn_pass(nxt + 5)
 
         n = N_GROUPS - 1
         t0 = n * TOKEN_TILES
@@ -449,19 +446,16 @@ def tile_attention_pa_kernel(
             rope_products(t0 + tt)
             rope_add((t0 + tt,), nc.gpsimd)
             sum_squares(t0 + tt)
-            root_mean_square(n, [tt])
+            invert_root(n, [tt])
         rope_products(t0 + 2)
         rope_products(t0 + 3)
         for tt in (2, 3):
-            rope_add((t0 + tt,), nc.vector)
+            rope_add((t0 + tt,), nc.gpsimd)
             sum_squares(t0 + tt)
-            root_mean_square(n, [tt])
-        invert(n, [0, 1])
+            invert_root(n, [tt])
         weigh_on_vector(2 * n, 0)
         normalise(t0)
         for tt in (1, 2, 3):
-            if tt > 1:
-                invert(n, [tt])
             finish_on_vector(t0 + tt)
             store(t0 + tt)
             if tt == 2:

@@ -129,6 +129,29 @@ def tile_attention_pa_kernel(
                 op=ALU.mult,
             )
 
+        def scale_by_vector(bank, grouped, g):
+            shape = [P, P, 2, 2]
+            nc.vector.tensor_tensor(
+                out=grouped[:, 0:512].rearrange("p (c u e) -> p c u e", u=2, e=2),
+                in0=bank[:, :, 0, :].bitcast(BF16).rearrange("p u (r e) -> p r u e", e=2),
+                in1=k_scale[:, g, :].rearrange("p (u e) -> p u e", e=2).unsqueeze(1).to_broadcast(shape),
+                op=ALU.mult,
+            )
+
+        def scale_by_scalar(bank, g):
+            planes = work.tile([P, 4, P], BF16, name="planes", bufs=2)
+            values = bank[:, :, 1, :].bitcast(BF16).rearrange("p u (r e) -> p u e r", e=2)
+            for t in range(4):
+                nc.scalar.activation(
+                    out=planes[:, t, :], in_=values[:, t // 2, t % 2, :], func=ACT.Copy, scale=k_scale[:, g, t : t + 1]
+                )
+            return planes
+
+        def interleave(planes, grouped):
+            nc.scalar.copy(
+                out=grouped[:, 512:1024].rearrange("p (c t) -> p c t", t=4), in_=planes[:].rearrange("p t c -> p c t")
+            )
+
         x_codes = const.tile([P, TOKEN_TILES, K_PASS], U32, name="x_codes", align_bytes=64)
         x_scales = const.tile([P, TOKEN_TILES, K_PASS], U8, name="x_scales", align_bytes=64)
         x_grouped = {}
@@ -387,7 +410,10 @@ def tile_attention_pa_kernel(
                     weigh(2 * n - 1, slice(tt - 2, tt - 1))
                     store(t0 - 4 + tt)
                 weigh_on_vector(2 * n - 2, 0)
+                planes = scale_by_scalar(banks_of[nxt][0], 0)
                 cast_half(4 * (n + 1) + 3)
+                empty_k(nxt)
+                interleave(planes, grouped_of[nxt])
             if halves:
                 cast_half(halves[0])
             if n > 0:
@@ -402,8 +428,11 @@ def tile_attention_pa_kernel(
                 widen_norm_weights()
             rope_add((t0, t0 + 1), nc.gpsimd)
             rope_add((t0 + 2, t0 + 3), nc.gpsimd)
-            empty_q(nxt)
-            empty_k(nxt)
+            if n > 0:
+                scale_by_vector(banks_of[nxt][0], grouped_of[nxt], 0)
+            else:
+                empty_q(nxt)
+                empty_k(nxt)
             turn_pass(nxt + 2)
             if n > 0:
                 for tt in (1, 0):

from contextlib import ExitStack

import concourse.mybir as mybir
from concourse.masks import make_identity

FLOPS = 2 * 512 * 4096 * 2048

F32 = mybir.dt.float32
BF16 = mybir.dt.bfloat16
U32 = mybir.dt.uint32
U8 = mybir.dt.uint8
FP8 = mybir.dt.float8_e4m3fn
FP8X4 = mybir.dt.float8_e4m3fn_x4
ALU = mybir.AluOpType
ACT = mybir.ActivationFunctionType

P = 128
K = 2048
K_PASS = 512
PASSES = K // K_PASS
TOKEN_TILES = 4
HEAD = 128
HALF = HEAD // 2
PAIR = 2
GROUP = 2 * PAIR * HEAD
N_GROUPS = 8
N_PASSES = N_GROUPS * PASSES
N_TILES = N_GROUPS * TOKEN_TILES
EPS = 2.0 ** -23
FINISH_ORDER = (2, 0, 1, 3)


def tile_attention_pa_kernel(
    tc, x, sin, cos, Wq_bytes, Wq_scale, Wk, q_norm_w, k_norm_w, out_0, out_1
):
    nc = tc.nc

    with ExitStack() as ctx:
        const = ctx.enter_context(tc.tile_pool(name="const", bufs=1))
        raw = ctx.enter_context(tc.tile_pool(name="raw", bufs=1))
        work = ctx.enter_context(tc.tile_pool(name="work", bufs=2))
        psum = ctx.enter_context(tc.psum_pool(name="psum", bufs=1))
        ctx.enter_context(tc.manual_schedule())

        k_scale = const.tile([P, PASSES, 4], F32, name="k_scale")
        nc.scalar.dma_start(out=k_scale[:], in_=Wq_scale.rearrange("o (g p t) -> p (o g) t", p=P, t=4))

        q_bytes = {}
        k_rows = {}
        x_flat = x.flatten_outer_dims()
        x_rows = []

        def load_group(i):
            rows = slice(i * PAIR * P, (i + 1) * PAIR * P)
            q_bytes[i] = raw.tile([P, PAIR, K], U8, name="q_bytes%d" % i)
            nc.sync.dma_start(out=q_bytes[i][:], in_=Wq_bytes[rows, :].rearrange("(r p) k -> p r k", p=P))
            k_rows[i] = raw.tile([P, PAIR, K], BF16, name="k_rows%d" % i)
            nc.sync.dma_start(out=k_rows[i][:], in_=Wk[rows, :].rearrange("(r p) k -> p r k", p=P))

        def load_x(tt):
            t = work.tile([P, K], BF16, name="x_rows", tag="rows", bufs=6)
            nc.sync.dma_start(out=t[:], in_=x_flat[tt * P : (tt + 1) * P, :])
            x_rows.append(t)

        q_bytes[0] = raw.tile([P, PAIR, K], U8, name="q_bytes0")
        k_half = []
        for half in range(2):
            k_half.append(raw.tile([P, PAIR, K // 2], BF16, name="k_half%d" % half))
        first = slice(0, PAIR * P)

        def load_first(tile, src, half):
            cols = slice(half * K // 2, (half + 1) * K // 2)
            nc.sync.dma_start(out=tile, in_=src[first, cols].rearrange("(r p) k -> p r k", p=P))

        rope_tab = const.tile([P, 2, 2, HEAD], BF16, name="rope_tab")
        norm_rows = const.tile([P, 2, HEAD], BF16, name="norm_rows")
        norm_wide = const.tile([P, 2, PAIR, HEAD], BF16, name="norm_wide")
        load_first(q_bytes[0][:, :, 0 : K // 2], Wq_bytes, 0)
        load_first(q_bytes[0][:, :, K // 2 : K], Wq_bytes, 1)
        load_first(k_half[0][:], Wk, 0)
        load_x(0)
        load_first(k_half[1][:], Wk, 1)
        load_x(1)
        nc.sync.dma_start(out=rope_tab[:, :, 1, 0:HALF], in_=sin.rearrange("(th p) j -> p th j", p=P))
        for w in range(2):
            nc.sync.dma_start(
                out=rope_tab[:, :, w, w * HALF : (w + 1) * HALF], in_=cos.rearrange("(th p) j -> p th j", p=P)
            )
        load_x(2)
        load_x(3)
        nc.sync.dma_start(out=norm_rows[:, 0, :], in_=q_norm_w.partition_broadcast(P))
        nc.sync.dma_start(out=norm_rows[:, 1, :], in_=k_norm_w.partition_broadcast(P))
        for i in range(1, N_GROUPS):
            load_group(i)

        ident = const.tile([P, P], F32, name="ident")
        make_identity(nc, ident[:])
        ident_bf = const.tile([P, P], BF16, name="ident_bf")
        make_identity(nc, ident_bf[:])

        zeros = const.tile([P, GROUP], BF16, name="zeros")
        nc.vector.memset(zeros[:], 0.0)

        one = const.tile([P, 1], F32, name="one")
        nc.vector.memset(one[:], 1.0)
        warm = const.tile([P, 1], F32, name="warm")
        nc.scalar.activation(out=warm[:], in_=one[:], func=ACT.Abs_reciprocal_sqrt)

        def turn(sources, tag="turned", bufs=4):
            bank = psum.tile([P, 2, 2, P], F32, name="turned", tag=tag, bufs=bufs)
            for s, (rows, g) in enumerate(sources):
                words = rows.bitcast(F32)
                for u in range(2):
                    nc.tensor.transpose(bank[:, u, s, :], words[:, 256 * g + u : 256 * (g + 1) : 2], ident[:])
            return bank

        def copy_out(engine_copy, bank, grouped, half):
            out_words = grouped[:, half * 1024 : (half + 1) * 1024].bitcast(F32)
            engine_copy(
                out=out_words.rearrange("p (c u) -> p c u", u=2), in_=bank[:].rearrange("p u s r -> p (s r) u")
            )

        def scale_out(bank, grouped, g):
            shape = [P, 2 * P, 2, 2]
            nc.vector.tensor_tensor(
                out=grouped[:, 0:1024].rearrange("p (c u e) -> p c u e", u=2, e=2),
                in0=bank[:].bitcast(BF16).rearrange("p u s (r e) -> p (s r) u e", e=2),
                in1=k_scale[:, g, :].rearrange("p (u e) -> p u e", e=2).unsqueeze(1).to_broadcast(shape),
                op=ALU.mult,
            )

        def scale_by_vector(bank, grouped, g):
            shape = [P, P, 2, 2]
            nc.vector.tensor_tensor(
                out=grouped[:, 0:512].rearrange("p (c u e) -> p c u e", u=2, e=2),
                in0=bank[:, :, 0, :].bitcast(BF16).rearrange("p u (r e) -> p r u e", e=2),
                in1=k_scale[:, g, :].rearrange("p (u e) -> p u e", e=2).unsqueeze(1).to_broadcast(shape),
                op=ALU.mult,
            )

        def scale_by_scalar(bank, g):
            planes = work.tile([P, 4, P], BF16, name="planes", bufs=2)
            values = bank[:, :, 1, :].bitcast(BF16).rearrange("p u (r e) -> p u e r", e=2)
            for t in range(4):
                nc.scalar.activation(
                    out=planes[:, t, :], in_=values[:, t // 2, t % 2, :], func=ACT.Copy, scale=k_scale[:, g, t : t + 1]
                )
            return planes

        def interleave(planes, grouped):
            nc.scalar.copy(
                out=grouped[:, 512:1024].rearrange("p (c t) -> p c t", t=4), in_=planes[:].rearrange("p t c -> p c t")
            )

        x_codes = const.tile([P, TOKEN_TILES, K_PASS], U32, name="x_codes", align_bytes=64)
        x_scales = const.tile([P, TOKEN_TILES, K_PASS], U8, name="x_scales", align_bytes=64)
        x_grouped = {}

        def turn_x(tt):
            grouped = work.tile([P, K], BF16, name="x_grouped", tag="grouped", bufs=8, align_bytes=64)
            rows = x_rows[tt][:]
            banks = ("acc", 3) if tt < 2 else ("turned", 4)
            copy_out(nc.scalar.copy, turn([(rows, 0), (rows, 1)], *banks), grouped, 0)
            copy_out(nc.scalar.copy, turn([(rows, 2), (rows, 3)], *banks), grouped, 1)
            x_grouped[tt] = grouped

        def quantise_x(tt):
            nc.vector.quantize_mx(
                out=x_codes[:, tt, :].bitcast(FP8X4), scales=x_scales[:, tt, :], in_=x_grouped[tt][:]
            )

        q_wide = {}

        def cast(copy, ci, part, parts):
            i, r = ci // PAIR, ci % PAIR
            if ci not in q_wide:
                q_wide[ci] = work.tile([P, K], BF16, name="q_wide", tag="rows", bufs=6)
            cols = slice(part * K // parts, (part + 1) * K // parts)
            copy(out=q_wide[ci][:, cols], in_=q_bytes[i][:, r, cols].bitcast(FP8))

        def cast_half(hi):
            i, j = hi // 4, hi % 4
            cast(nc.scalar.copy, PAIR * i + j % 2, j // 2, 2)

        grouped_of = {}
        banks_of = {}
        codes_of = {}

        def turn_q(pi):
            i, g = pi // PASSES, pi % PASSES
            grouped_of[pi] = work.tile([P, K], BF16, name="grouped", tag="grouped", bufs=8, align_bytes=64)
            banks_of[pi] = [turn([(q_wide[PAIR * i][:], g), (q_wide[PAIR * i + 1][:], g)])]

        def turn_k(pi):
            i, g = pi // PASSES, pi % PASSES
            rows, gg = (k_rows[i], g) if i > 0 else (k_half[g // 2], g % 2)
            banks_of[pi].append(turn([(rows[:, 0, :], gg), (rows[:, 1, :], gg)]))

        def turn_pass(pi):
            turn_q(pi)
            turn_k(pi)

        def empty_q(pi):
            scale_out(banks_of[pi][0], grouped_of[pi], pi % PASSES)

        def empty_k(pi):
            copy_out(nc.scalar.copy, banks_of[pi][1], grouped_of[pi], 1)

        def quantise_pass(pi):
            i, g = pi // PASSES, pi % PASSES
            if g == 0:
                codes = work.tile([P, PASSES, GROUP], U32, name="w_codes", bufs=2, align_bytes=64)
                scales = work.tile([P, PASSES, GROUP], U8, name="w_scales", bufs=2, align_bytes=64)
                codes_of[i] = (codes, scales)
            codes, scales = codes_of[i]
            nc.vector.quantize_mx(
                out=codes[:, g, :].bitcast(FP8X4), scales=scales[:, g, :], in_=grouped_of[pi][:]
            )

        acc_of = {}

        def keep_warm(times):
            bank = psum.tile([P, GROUP], F32, name="warm_bank", tag="acc", bufs=3)
            for r in range(times):
                nc.tensor.matmul(out=bank[:], lhsT=ident_bf[:], rhs=zeros[:], start=True, stop=True)

        def multiply(ti):
            i, tt = ti // TOKEN_TILES, ti % TOKEN_TILES
            codes, scales = codes_of[i]
            acc = psum.tile([P, GROUP], F32, name="acc", tag="acc", bufs=3)
            for g in range(PASSES):
                tok = slice(g * P, (g + 1) * P)
                nc.tensor.matmul_mx(
                    out=acc[:],
                    lhsT=x_codes[:, tt, tok].bitcast(FP8X4),
                    lhsT_scale=x_scales[:, tt, tok],
                    rhs=codes[:, g, :].bitcast(FP8X4),
                    rhs_scale=scales[:, g, :],
                    start=(g == 0),
                    stop=(g == PASSES - 1),
                )
            acc_of[ti] = acc

        prod_of = {}
        roped_of = {}
        sumsq_of = {}
        inv_of = {}

        def rope_products(ti):
            shape = [P, 2, 2 * PAIR, HEAD]
            if ti % 2 == 0 or ti > N_TILES - TOKEN_TILES:
                prod_of[ti] = work.tile([P, 2, 2, GROUP], F32, name="prod", bufs=3)
            else:
                prod_of[ti] = prod_of[ti - 1]
            nc.vector.tensor_tensor(
                out=prod_of[ti][:, :, ti % 2, :].rearrange("p w (h d) -> p w h d", d=HEAD),
                in0=acc_of[ti][:].rearrange("p (h d) -> p h d", d=HEAD).unsqueeze(1).to_broadcast(shape),
                in1=rope_tab[:, ti % 2, :, :].unsqueeze(2).to_broadcast(shape),
                op=ALU.mult,
            )

        def rope_add(tiles, adder):
            pr, ts = tiles[0] // 2, slice(tiles[0] % 2, tiles[-1] % 2 + 1)
            if ts.start == 0:
                roped_of[pr] = work.tile([P, 2, GROUP], F32, name="roped", bufs=5)
            halves = prod_of[tiles[0]][:, :, ts, :].rearrange("p w t (h f j) -> p w (t h) f j", f=2, j=HALF)
            adder.tensor_tensor(
                out=roped_of[pr][:, ts, :].rearrange("p t (h w j) -> p w (t h) j", w=2, j=HALF),
                in0=halves[:, :, :, 0, :],
                in1=halves[:, :, :, 1, :],
                op=ALU.add,
            )

        def column(tt):
            return 4 * FINISH_ORDER.index(tt)

        def columns(tts):
            return slice(column(tts[0]), column(tts[-1]) + 4)

        def sum_squares(ti):
            i, tt = ti // TOKEN_TILES, ti % TOKEN_TILES
            if tt == 0:
                sumsq_of[i] = work.tile([P, 4 * TOKEN_TILES], F32, name="sumsq", bufs=3)
                inv_of[i] = work.tile([P, 4 * TOKEN_TILES], F32, name="inv", bufs=3)
            for h in range(2 * PAIR):
                squares = work.tile([P, HEAD], BF16, name="squares", bufs=16)
                col = column(tt) + h
                nc.scalar.activation(
                    out=squares[:],
                    in_=roped_of[ti // 2][:, ti % 2, h * HEAD : (h + 1) * HEAD],
                    func=ACT.Square,
                    accum_out=sumsq_of[i][:, col : col + 1],
                )

        def invert_root(i, tts):
            cols = columns(tts)
            nc.scalar.activation(
                out=inv_of[i][:, cols], in_=sumsq_of[i][:, cols], func=ACT.Abs_reciprocal_sqrt, bias=EPS, scale=1.0 / HEAD
            )

        def weigh(pr, tts, cols=slice(0, GROUP)):
            part = roped_of[pr][:, tts, cols]
            rows = norm_wide[:].rearrange("p m h d -> p (m h d)")[:, cols]
            shape = [P, tts.stop - tts.start, cols.stop - cols.start]
            nc.gpsimd.tensor_tensor(out=part, in0=part, in1=rows.unsqueeze(1).to_broadcast(shape), op=ALU.mult)

        def weigh_on_vector(pr, t):
            part = roped_of[pr][:, t, :]
            nc.vector.tensor_tensor(
                out=part, in0=part, in1=norm_bank[:].rearrange("p m h d -> p (m h d)"), op=ALU.mult
            )

        def normalise(ti):
            i, tt = ti // TOKEN_TILES, ti % TOKEN_TILES
            roped = roped_of[ti // 2][:, ti % 2, :]
            for h in range(2 * PAIR):
                cols = slice(h * HEAD, (h + 1) * HEAD)
                inv = inv_of[i][:, column(tt) + h : column(tt) + h + 1]
                nc.scalar.activation(out=roped[:, cols], in_=roped[:, cols], func=ACT.Copy, scale=inv)

        def finish_on_vector(ti):
            i, tt = ti // TOKEN_TILES, ti % TOKEN_TILES
            roped = roped_of[ti // 2][:, ti % 2, :]
            for h in range(2 * PAIR):
                cols = slice(h * HEAD, (h + 1) * HEAD)
                inv = inv_of[i][:, column(tt) + h : column(tt) + h + 1]
                nc.vector.scalar_tensor_tensor(
                    out=roped[:, cols], in0=roped[:, cols], scalar=inv, in1=norm_bank[:, h // PAIR, h % PAIR, :],
                    op0=ALU.mult, op1=ALU.mult,
                )

        def store(ti):
            i, tt = ti // TOKEN_TILES, ti % TOKEN_TILES
            b, th = tt // 2, tt % 2
            for m, dst in enumerate((out_0, out_1)):
                nc.sync.dma_start(
                    out=dst[b, i * PAIR : (i + 1) * PAIR, th * P : (th + 1) * P, :].rearrange("h t d -> t h d"),
                    in_=roped_of[ti // 2][:, ti % 2, m * PAIR * HEAD : (m + 1) * PAIR * HEAD].rearrange("p (h d) -> p h d", d=HEAD),
                )

        def widen_norm_weights():
            for h in range(PAIR):
                nc.scalar.copy(out=norm_wide[:, :, h, :], in_=norm_rows[:])

        def park_norm_weights():
            for m in range(2):
                for h in range(PAIR):
                    nc.tensor.matmul(
                        out=norm_bank[:, m, h, :], lhsT=ident_bf[:], rhs=norm_rows[:, m, :], start=True, stop=True
                    )

        norm_bank = psum.tile([P, 2, PAIR, HEAD], F32, name="norm_bank", tag="norm_bank", bufs=1)

        for g in range(PASSES):
            for r in range(PAIR):
                cast(nc.vector.tensor_copy if g < 2 else nc.scalar.copy, r, g, PASSES)
        nc.gpsimd.tensor_scalar(
            out=rope_tab[:, :, 0, HALF:HEAD], in0=rope_tab[:, :, 1, 0:HALF], scalar1=-1.0, scalar2=0.0, op0=ALU.mult, op1=ALU.add
        )
        turn_q(0)
        turn_q(1)
        turn_q(2)
        turn_q(3)
        for g in range(PASSES):
            empty_q(g)
        turn_k(0)
        turn_k(1)
        empty_k(0)
        empty_k(1)
        turn_x(0)
        turn_k(2)
        turn_k(3)
        empty_k(2)
        empty_k(3)
        quantise_x(0)
        turn_x(1)
        turn_x(2)
        turn_x(3)

        for n in range(N_GROUPS):
            t0 = n * TOKEN_TILES
            nxt = (n + 1) * PASSES if n + 1 < N_GROUPS else None
            halves = [4 * (n + 2) + h for h in range(4)] if n + 2 < N_GROUPS else []
            last = n == N_GROUPS - 1
            for g in range(PASSES):
                quantise_pass(n * PASSES + g)
            multiply(t0)
            if n == 0:
                for h in range(4, 8):
                    cast_half(h)
                for tt in (1, 2, 3):
                    quantise_x(tt)
                multiply(t0 + 1)
                multiply(t0 + 2)
                rope_products(t0)
                multiply(t0 + 3)
                rope_products(t0 + 1)
                rope_products(t0 + 2)
                turn_pass(4)
                turn_pass(5)
                park_norm_weights()
            else:
                multiply(t0 + 1)
                multiply(t0 + 2)
            if last:
                continue
            if n > 0:
                for tt in (2, 3):
                    normalise(t0 - 4 + tt)
                    weigh(2 * n - 1, slice(tt - 2, tt - 1))
                    store(t0 - 4 + tt)
                weigh_on_vector(2 * n - 2, 0)
                planes = scale_by_scalar(banks_of[nxt][0], 0)
                cast_half(4 * (n + 1) + 3)
                empty_k(nxt)
                interleave(planes, grouped_of[nxt])
            if halves:
                cast_half(halves[0])
            if n > 0:
                rope_products(t0)
                multiply(t0 + 3)
                turn_pass(nxt + 1)
                keep_warm(2)
                for tt in (1, 2, 3):
                    rope_products(t0 + tt)
            else:
                rope_products(t0 + 3)
                widen_norm_weights()
            rope_add((t0, t0 + 1), nc.gpsimd)
            rope_add((t0 + 2, t0 + 3), nc.gpsimd)
            if n > 0:
                scale_by_vector(banks_of[nxt][0], grouped_of[nxt], 0)
            else:
                empty_q(nxt)
                empty_k(nxt)
            turn_pass(nxt + 2)
            if n > 0:
                for tt in (1, 0):
                    normalise(t0 - 4 + tt)
                    store(t0 - 4 + tt)
            if halves:
                cast_half(halves[1])
            empty_q(nxt + 1)
            empty_k(nxt + 1)
            turn_pass(nxt + 3)
            sum_squares(t0)
            sum_squares(t0 + 1)
            weigh(2 * n, slice(1, 2))
            empty_q(nxt + 2)
            empty_k(nxt + 2)
            empty_q(nxt + 3)
            sum_squares(t0 + 2)
            empty_k(nxt + 3)
            invert_root(n, [2])
            sum_squares(t0 + 3)
            if halves:
                cast_half(halves[2])
            invert_root(n, [0, 1, 3])
            if n + 2 < N_GROUPS:
                turn_pass(nxt + 4)

        n = N_GROUPS - 1
        t0 = n * TOKEN_TILES
        multiply(t0 + 3)
        normalise(t0 - 2)
        weigh(2 * n - 1, slice(0, 1))
        finish_on_vector(t0 - 1)
        for tt in (-1, -2):
            store(t0 + tt)
        weigh_on_vector(2 * n - 2, 0)
        for tt in (1, 0):
            normalise(t0 - 4 + tt)
            store(t0 - 4 + tt)
        for tt in (0, 1):
            rope_products(t0 + tt)
            rope_add((t0 + tt,), nc.gpsimd)
            sum_squares(t0 + tt)
            invert_root(n, [tt])
        rope_products(t0 + 2)
        rope_products(t0 + 3)
        for tt in (2, 3):
            rope_add((t0 + tt,), nc.gpsimd)
            sum_squares(t0 + tt)
            invert_root(n, [tt])
        weigh_on_vector(2 * n, 0)
        normalise(t0)
        for tt in (1, 2, 3):
            finish_on_vector(t0 + tt)
            store(t0 + tt)
            if tt == 2:
                store(t0)
